import numpy as np
import ml_dtypes


def mxq(x, axis, fmt="e4m3"):
    dtype, down = {"e4m3": (ml_dtypes.float8_e4m3fn, 7), "e5m2": (ml_dtypes.float8_e5m2, 14)}[fmt]
    v = np.moveaxis(np.asarray(x, np.float32).astype(ml_dtypes.bfloat16).astype(np.float64), axis, -1)
    blocks = v.reshape(v.shape[:-1] + (-1, 32))
    amax = np.abs(blocks).max(-1, keepdims=True)
    byte = np.maximum(np.where(amax > 0, np.frexp(amax)[1] - 1 + 127, 0) - down, 1)
    scale = np.exp2(byte - 127.0)
    codes = (blocks / scale).astype(np.float32).astype(dtype).astype(np.float64)
    return np.moveaxis((codes * scale).reshape(v.shape), -1, axis)


WIDE = False


def mx_kscale(k):
    if not WIDE:
        return np.ones(k)
    levels = np.array([10, -10, 5, -5, 0])
    if k % 512:
        return np.exp2(np.random.permutation(np.resize(levels, k // 32))).repeat(32)
    a = np.empty((k // 512, 16))
    for p in range(k // 512):
        a[p, :8] = np.random.permutation(np.resize(levels, 8))
        for g in range(8):
            far = levels[np.abs(levels - a[p, g]) >= 10]
            a[p, g + 8] = far[np.random.randint(len(far))]
    return np.exp2(a.ravel()).repeat(32)


BF16 = ml_dtypes.bfloat16


def bf(x):
    return np.asarray(x, np.float32).astype(BF16)


def f64(x):
    return np.asarray(x).astype(np.float64)


B, H0, C0, C1, C2, NA, NO = 2, 32, 512, 512, 1024, 3, 128
H1, H2 = H0 // 2, H0 // 4
O = NA * NO


def sigmoid(v):
    return 1.0 / (1.0 + np.exp(-v))


def _draw_level(c, h):
    s = mx_kscale(c)
    f = bf(np.random.standard_normal((B, c, h, h)) * s[None, :, None, None])
    w = bf(np.random.standard_normal((O, c)) / np.sqrt(c) / s[None, :])
    b = bf(np.random.standard_normal(O) * 0.5)
    return f, w, b


def setup_inputs():
    f0, w0, b0 = _draw_level(C0, H0)
    f1, w1, b1 = _draw_level(C1, H1)
    f2, w2, b2 = _draw_level(C2, H2)
    anchors = bf(1.0 + 4.0 * np.random.random((3, NA, 2)))
    return {"f0": f0, "f1": f1, "f2": f2, "w0": w0, "b0": b0, "w1": w1, "b1": b1, "w2": w2, "b2": b2, "anchors": anchors}


def _decode_level(f, w, b, anchors_i):
    nb, c, h, wd = f.shape
    y = (mxq(w, 1, "e4m3") @ mxq(f.reshape(nb, c, h * wd), 1, "e4m3")) + b[None, :, None]
    y = y.reshape(nb, NA, NO, h, wd).transpose(0, 1, 3, 4, 2)
    xy = 2.0 * sigmoid(y[..., 0:2]) - 0.5
    wh = np.square(2.0 * sigmoid(y[..., 2:4])) * anchors_i[None, :, None, None, :]
    rest = y[..., 4:]
    out = np.concatenate([xy, wh, rest], axis=-1)
    return out.reshape(nb, -1, NO)


def core(f0, f1, f2, w0, b0, w1, b1, w2, b2, anchors):
    a = f64(anchors)
    outs = [
        _decode_level(f64(f0), f64(w0), f64(b0), a[0]),
        _decode_level(f64(f1), f64(w1), f64(b1), a[1]),
        _decode_level(f64(f2), f64(w2), f64(b2), a[2]),
    ]
    return np.concatenate(outs, axis=1)


def e4m3fn_bytes(y):
    return np.clip(np.asarray(y, np.float64), -448.0, 448.0).astype(np.float32).astype(ml_dtypes.float8_e4m3fn).view(np.uint8)


Y_SCALE = 190.0


def reference(f0, f1, f2, w0, b0, w1, b1, w2, b2, anchors):
    out = core(f0, f1, f2, w0, b0, w1, b1, w2, b2, anchors)
    return out, e4m3fn_bytes(out * Y_SCALE)

@@ -1,0 +1,389 @@
+from contextlib import ExitStack
+
+import concourse.mybir as mybir
+from concourse.masks import make_identity
+
+FLOPS = 1107296256
+
+F32 = mybir.dt.float32
+BF16 = mybir.dt.bfloat16
+I32 = mybir.dt.int32
+U32 = mybir.dt.uint32
+U8 = mybir.dt.uint8
+FP8X4 = mybir.dt.float8_e4m3fn_x4
+FP8 = mybir.dt.float8_e4m3fn
+ACT = mybir.ActivationFunctionType
+ALU = mybir.AluOpType
+
+P = 128
+NA = 3
+NO = 128
+Y_SCALE = 190.0
+MANUAL = False
+
+
+def tile_head_kernel(tc, f0, f1, f2, w0, b0, w1, b1, w2, b2, anchors, out_0, out_1):
+    nc = tc.nc
+    with ExitStack() as ctx:
+        keep = ctx.enter_context(tc.tile_pool(name="keep", bufs=1))
+        ps_mm = ctx.enter_context(tc.psum_pool(name="ps_mm", bufs=6))
+        ps_xt = ctx.enter_context(tc.psum_pool(name="ps_xt", bufs=2))
+        if MANUAL:
+            ctx.enter_context(tc.manual_schedule())
+
+        raw00 = keep.tile([P, 4, 512], BF16, name="raw00")
+        raw01 = keep.tile([P, 4, 512], BF16, name="raw01")
+        raw1x = keep.tile([P, 4, 1024], BF16, name="raw1x")
+        wr0 = keep.tile([P, NA, 512], BF16, name="wr0")
+        wr1 = keep.tile([P, NA, 512], BF16, name="wr1")
+        wr2 = keep.tile([P, NA, 1024], BF16, name="wr2")
+        rawl1 = keep.tile([P, 2, 4, 256], BF16, name="rawl1")
+        rawl2 = keep.tile([P, 2, 2, 4, 64], BF16, name="rawl2")
+        f0n0 = f0[0].rearrange("(p j) u v -> p j (u v)", j=4)
+        f0n1 = f0[1].rearrange("(p j) u v -> p j (u v)", j=4)
+        nc.sync.dma_start(out=raw00[:], in_=f0n0[:, :, 0:512])
+        nc.sync.dma_start(out=wr0[:], in_=w0.rearrange("(a r) k -> r a k", a=NA))
+        nc.sync.dma_start(out=raw01[:], in_=f0n0[:, :, 512:1024])
+        nc.sync.dma_start(out=raw1x[:], in_=f0n1)
+        nc.sync.dma_start(out=wr1[:], in_=w1.rearrange("(a r) k -> r a k", a=NA))
+        nc.sync.dma_start(
+            out=rawl1[:].rearrange("p n j x -> p n (j x)"),
+            in_=f1.rearrange("n (p j) u v -> p n (j u v)", j=4),
+        )
+        nc.sync.dma_start(out=wr2[:], in_=w2.rearrange("(a r) k -> r a k", a=NA))
+        for n in range(2):
+            nc.sync.dma_start(
+                out=rawl2[:, n].rearrange("p k j x -> p k (j x)"),
+                in_=f2[n].rearrange("(k p j) u v -> p k (j u v)", k=2, j=4),
+            )
+
+        rows = keep.tile([P, 1056], BF16, name="rows")
+        nc.vector.memset(rows[:].bitcast(I32), 0)
+        warm = keep.tile([P, 2], F32, name="warm")
+        nc.vector.memset(warm[:], 0.0)
+        anc = anchors.rearrange("(o l) a w -> o (l a w)", o=1)
+        nc.scalar.dma_start(out=rows[0:1, 0:384], in_=b0.rearrange("(o c) -> o c", o=1))
+        nc.scalar.dma_start(out=rows[0:1, 1024:1042], in_=anc)
+        nc.scalar.dma_start(out=rows[0:1, 384:768], in_=b1.rearrange("(o c) -> o c", o=1))
+        nc.scalar.dma_start(out=rows[0:1, 768:1024], in_=b2[0:256].rearrange("(o c) -> o c", o=1))
+        nc.scalar.dma_start(out=rows[64:65, 768:1024], in_=b2[128:384].rearrange("(o c) -> o c", o=1))
+        nc.scalar.dma_start(out=rows[64:65, 1036:1040], in_=anc[:, 14:18])
+        nc.scalar.activation(out=warm[:, 1:2], in_=warm[:, 0:1], func=ACT.Sigmoid)
+
+        ones = keep.tile([P, P], BF16, name="ones")
+        halves = keep.tile([P, P], BF16, name="halves")
+        ident = keep.tile([P, P], F32, name="ident")
+        nc.gpsimd.memset(ones[:], 1.0)
+        nc.gpsimd.memset(halves[:], 0.0)
+        nc.gpsimd.memset(halves[0:64, 0:64], 1.0)
+        nc.gpsimd.memset(halves[64:128, 64:128], 1.0)
+        make_identity(nc, ident[:])
+
+        fg2 = keep.tile([P, 8, 64, 4], BF16, name="fg2", align_bytes=64)
+        nc.gpsimd.memset(fg2[:], 0.0)
+        fq2 = keep.tile([P, 576], U32, name="fq2", align_bytes=64)
+        fs2 = keep.tile([P, 576], U8, name="fs2", align_bytes=64)
+        nc.vector.memset(fq2[:, 512:576].bitcast(I32), 0)
+        nc.vector.memset(fs2[:, 512:576].bitcast(I32), 0)
+
+        pb = ps_xt.tile([P, 1024], BF16, tag="xt")
+        nc.tensor.matmul(out=pb[:, 0:384], lhsT=ones[:], rhs=rows[:, 0:384], start=True, stop=True)
+        nc.tensor.matmul(out=pb[:, 384:768], lhsT=ones[:], rhs=rows[:, 384:768], start=True, stop=True)
+        nc.tensor.matmul(out=pb[:, 768:1024], lhsT=halves[:], rhs=rows[:, 768:1024], start=True, stop=True)
+        pa = ps_xt.tile([P, 16], F32, tag="xt")
+        nc.tensor.matmul(out=pa[:, 0:12], lhsT=ones[:], rhs=rows[:, 1024:1036], start=True, stop=True)
+        nc.tensor.matmul(out=pa[:, 12:16], lhsT=halves[:], rhs=rows[:, 1036:1040], start=True, stop=True)
+        bias = keep.tile([P, 1024], BF16, name="bias")
+        nc.scalar.copy(out=bias[:], in_=pb[:])
+        a4 = keep.tile([P, 2, NA, 4, 2], F32, name="a4")
+        for lv in range(2):
+            nc.scalar.activation(
+                out=a4[:, lv],
+                in_=pa[:, 6 * lv : 6 * lv + 6]
+                .rearrange("p (a w) -> p a w", w=2)
+                .unsqueeze(2)
+                .to_broadcast([P, NA, 4, 2]),
+                func=ACT.Copy,
+                scale=4.0,
+            )
+        a42 = keep.tile([P, 2, 4], F32, name="a42")
+        nc.scalar.activation(
+            out=a42[:], in_=pa[:, 12:16].unsqueeze(1).to_broadcast([P, 2, 4]), func=ACT.Copy, scale=4.0
+        )
+
+        wraws = [wr0, wr1, wr2]
+        wq = []
+        ws = []
+        wgs = []
+        for lv in range(3):
+            units = 3 if lv < 2 else 6
+            wg_t = keep.tile([P, units, NO, 4], BF16, name="wg%d" % lv, align_bytes=64)
+            wq_t = keep.tile([P, units * NO], U32, name="wq%d" % lv, align_bytes=64)
+            ws_t = keep.tile([P, units * NO], U8, name="ws%d" % lv, align_bytes=64)
+            wgs.append(wg_t)
+            wq.append(wq_t)
+            ws.append(ws_t)
+
+        def weights_turn(lv, q0, nq):
+            words = wraws[lv][:].bitcast(F32)
+            xt = ps_xt.tile([P, 2, 2, NO], F32, tag="xt")
+            for i in range(nq):
+                kp, a = divmod(q0 + i, NA)
+                for u in range(2):
+                    nc.tensor.transpose(
+                        xt[:, i, u, :], words[:, a, 256 * kp + u : 256 * (kp + 1) : 2], ident[:]
+                    )
+            nc.scalar.copy(
+                out=wgs[lv][:].bitcast(F32)[:, q0 : q0 + nq],
+                in_=xt[:, 0:nq].rearrange("p i u r -> p i r u"),
+            )
+
+        def weights_quant(lv, q0, nq):
+            flat = wgs[lv][:].rearrange("p q r t -> p (q r t)")
+            nc.vector.quantize_mx(
+                out=wq[lv][:, q0 * NO : (q0 + nq) * NO].bitcast(FP8X4),
+                scales=ws[lv][:, q0 * NO : (q0 + nq) * NO],
+                in_=flat[:, q0 * 4 * NO : (q0 + nq) * 4 * NO],
+            )
+
+        fg = []
+        fq = []
+        fs = []
+        ot = []
+        qt = []
+        for c in range(5):
+            fg_t = keep.tile([P, 4, P, 4], BF16, name="fg_%d" % c, align_bytes=64)
+            fq_t = keep.tile([P, 512], U32, name="fq_%d" % c, align_bytes=64)
+            fs_t = keep.tile([P, 512], U8, name="fs_%d" % c, align_bytes=64)
+            o_t = keep.tile([P, NA, 4, NO], F32, name="o_%d" % c)
+            q_t = keep.tile([P, NA * 4 * NO], FP8, name="q_%d" % c)
+            fg.append(fg_t)
+            fq.append(fq_t)
+            fs.append(fs_t)
+            ot.append(o_t)
+            qt.append(q_t)
+        o2 = keep.tile([P, 4, NO], F32, name="o_5")
+        q2 = keep.tile([P, 4 * NO], FP8, name="q_5")
+        fg.append(fg2)
+        fq.append(fq2)
+        fs.append(fs2)
+        ot.append(o2)
+        qt.append(q2)
+
+        def pieces(c):
+            if c < 4:
+                src = [raw00[:], raw01[:], raw1x[:, :, 0:512], raw1x[:, :, 512:1024]][c]
+                sv = src.rearrange("p j (m g) -> p g m j", g=4)
+                return [(fg[c][:, g : g + 1], sv[:, g : g + 1]) for g in range(4)]
+            if c == 4:
+                res = []
+                for n in range(2):
+                    sv = rawl1[:, n].rearrange("p j (m g) -> p g m j", g=2)
+                    for g in range(2):
+                        res.append((fg[c][:, 2 * n + g : 2 * n + g + 1], sv[:, g : g + 1]))
+                return res
+            dst = fg2[:].rearrange("p (q z) x j -> p q z x j", z=2)[:, :, 1]
+            sv = rawl2[:].rearrange("p n k j x -> p (n k) x j")
+            return [(dst[:, 0:2], sv[:, 0:2]), (dst[:, 2:4], sv[:, 2:4])]
+
+        def inter_v(c):
+            pc = pieces(c)
+            if c < 4:
+                src = [raw00[:], raw01[:], raw1x[:, :, 0:512], raw1x[:, :, 512:1024]][c]
+                sv = src.rearrange("p j (m g) -> p g m j", g=4)
+                nc.vector.tensor_copy(out=fg[c][:, 0:2], in_=sv[:, 0:2])
+            elif c == 4:
+                sv = rawl1[:, 0].rearrange("p j (m g) -> p g m j", g=2)
+                nc.vector.tensor_copy(out=fg[c][:, 0:2], in_=sv)
+            else:
+                nc.vector.tensor_copy(out=pc[0][0], in_=pc[0][1])
+
+        def inter_s(c, part):
+            pc = pieces(c)
+            if c < 5:
+                nc.scalar.copy(out=pc[2 + part][0], in_=pc[2 + part][1])
+            elif part == 0:
+                nc.scalar.copy(out=pc[1][0], in_=pc[1][1])
+
+        def quant(c):
+            if c < 5:
+                flat = fg[c][:].rearrange("p g m j -> p (g m j)")
+            else:
+                flat = fg2[:].rearrange("p b x j -> p (b x j)")
+            nc.vector.quantize_mx(out=fq[c][:, 0:512].bitcast(FP8X4), scales=fs[c][:, 0:512], in_=flat)
+
+        banks = {}
+
+        def mm(c):
+            if c < 5:
+                lv = 0 if c < 4 else 1
+                for a in range(NA):
+                    acc = ps_mm.tile([P, 4, NO], F32, tag="acc")
+                    for s in range(4):
+                        nc.tensor.matmul_mx(
+                            out=acc[:, s, :],
+                            lhsT=fq[c][:, s * P : (s + 1) * P].bitcast(FP8X4),
+                            lhsT_scale=fs[c][:, s * P : (s + 1) * P],
+                            rhs=wq[lv][:, a * NO : (a + 1) * NO].bitcast(FP8X4),
+                            rhs_scale=ws[lv][:, a * NO : (a + 1) * NO],
+                            start=True,
+                            stop=True,
+                        )
+                    banks[(c, a)] = acc
+            else:
+                acc = ps_mm.tile([P, 4, NO], F32, tag="acc")
+                for n in range(2):
+                    for t in range(2):
+                        todo = []
+                        for half in range(2):
+                            for kp in range(2):
+                                todo.append(((2 * (2 * n + kp) + 1 - half) * 64, (kp * NA + t + half) * NO))
+                        for i in range(4):
+                            fc, wc = todo[i]
+                            nc.tensor.matmul_mx(
+                                out=acc[:, 2 * n + t, :],
+                                lhsT=fq2[:, fc : fc + P].bitcast(FP8X4),
+                                lhsT_scale=fs2[:, fc : fc + P],
+                                rhs=wq[2][:, wc : wc + NO].bitcast(FP8X4),
+                                rhs_scale=ws[2][:, wc : wc + NO],
+                                start=(i == 0),
+                                stop=(i == 3),
+                            )
+                banks[(c, 0)] = acc
+
+        def badd(c):
+            if c < 5:
+                off = 0 if c < 4 else 384
+                for a in range(NA):
+                    nc.vector.tensor_tensor(
+                        out=ot[c][:, a],
+                        in0=banks[(c, a)][:],
+                        in1=bias[:, off + a * NO : off + (a + 1) * NO].unsqueeze(1).to_broadcast([P, 4, NO]),
+                        op=ALU.add,
+                    )
+            else:
+                nc.vector.tensor_tensor(
+                    out=o2[:].rearrange("p (n t) j -> p n (t j)", n=2),
+                    in0=banks[(c, 0)][:].rearrange("p (n t) j -> p n (t j)", n=2),
+                    in1=bias[:, 768:1024].unsqueeze(1).to_broadcast([P, 2, 2 * NO]),
+                    op=ALU.add,
+                )
+
+        sgs = {}
+
+        def rows_of(c):
+            if c < 5:
+                return ot[c][:].rearrange("p a s j -> p (a s) j")
+            return o2[:]
+
+        def sig(c):
+            nr = 12 if c < 5 else 4
+            sg = keep.tile([P, nr, 4], F32, name="sg%d" % c)
+            nc.scalar.activation(out=sg[:], in_=rows_of(c)[:, :, 0:4], func=ACT.Sigmoid)
+            sgs[c] = sg
+
+        def fixv(c):
+            nr = 12 if c < 5 else 4
+            sg = sgs[c]
+            rv = rows_of(c)
+            if c < 5:
+                av = a4[:, 0 if c < 4 else 1].rearrange("p a g w -> p (a g) w")
+            else:
+                av = a42[:].rearrange("p n (t w) -> p (n t) w", w=2)
+            sa = keep.tile([P, nr, 2], F32, name="sa%d" % c)
+            nc.vector.tensor_tensor(out=sa[:], in0=sg[:, :, 2:4], in1=av, op=ALU.mult)
+            nc.vector.tensor_scalar(
+                out=rv[:, :, 0:2], in0=sg[:, :, 0:2], scalar1=2.0, scalar2=-0.5, op0=ALU.mult, op1=ALU.add
+            )
+            nc.vector.tensor_tensor(out=rv[:, :, 2:4], in0=sa[:], in1=sg[:, :, 2:4], op=ALU.mult)
+
+        def cast(c, part, on_vector=False):
+            if c < 5:
+                src = ot[c][:].rearrange("p a s j -> p (a s j)")[:, part * 512 : (part + 1) * 512]
+                dst = qt[c][:, part * 512 : (part + 1) * 512]
+            else:
+                src = o2[:].rearrange("p t j -> p (t j)")
+                dst = q2[:]
+            if on_vector:
+                nc.vector.tensor_scalar(
+                    out=dst, in0=src, scalar1=Y_SCALE, scalar2=None, op0=ALU.mult, saturate=False
+                )
+            else:
+                nc.scalar.activation(out=dst, in_=src, func=ACT.Copy, scale=Y_SCALE, saturate=False)
+
+        def dests(c, out):
+            if c < 4:
+                n, h = divmod(c, 2)
+                v = out[n, 0:3072, :].rearrange("(a h m g) j -> h m a (g j)", a=NA, h=2, m=P, g=4)
+                return [v[h]]
+            if c == 4:
+                return [
+                    out[n, 3072:3840, :].rearrange("(a m g) j -> m a (g j)", a=NA, m=P, g=2) for n in range(2)
+                ]
+            return [out[:, 3840 + 64 * t : 3968 + 64 * t, :].rearrange("n m j -> m n j") for t in range(2)]
+
+        def sources(c, tile_ap):
+            if c < 4:
+                return [tile_ap.rearrange("p (a x) -> p a x", a=NA)]
+            if c == 4:
+                v = tile_ap.rearrange("p (a n x) -> p n a x", a=NA, n=2)
+                return [v[:, n] for n in range(2)]
+            v = tile_ap.rearrange("p (n t j) -> p t n j", n=2, t=2)
+            return [v[:, t] for t in range(2)]
+
+        def store0(c):
+            if c < 5:
+                flat = ot[c][:].rearrange("p a s j -> p (a s j)")
+            else:
+                flat = o2[:].rearrange("p t j -> p (t j)")
+            ds = dests(c, out_0)
+            ss = sources(c, flat)
+            for i in range(len(ds)):
+                nc.sync.dma_start(out=ds[i], in_=ss[i])
+
+        def store1(c):
+            ds = dests(c, out_1)
+            ss = sources(c, qt[c][:].bitcast(U8))
+            for i in range(len(ds)):
+                nc.sync.dma_start(out=ds[i], in_=ss[i])
+
+        for c in range(-2, 7):
+            if 0 <= c + 1 < 6:
+                quant(c + 1)
+            if c == -1:
+                weights_quant(0, 0, 2)
+                weights_quant(0, 2, 1)
+            if 0 <= c + 1 < 6:
+                mm(c + 1)
+            if 0 <= c - 1 < 6:
+                store0(c - 1)
+                for part in range(3 if c - 1 < 5 else 1):
+                    cast(c - 1, part)
+                store1(c - 1)
+            if c == 1:
+                weights_turn(1, 0, 2)
+                weights_turn(1, 2, 1)
+            if c == 2:
+                weights_turn(2, 0, 2)
+                weights_turn(2, 2, 2)
+                weights_turn(2, 4, 2)
+            if 0 <= c < 6:
+                badd(c)
+            if c == 1:
+                weights_quant(1, 0, 2)
+                weights_quant(1, 2, 1)
+            if c == 2:
+                weights_quant(2, 0, 4)
+                weights_quant(2, 4, 2)
+            if 0 <= c + 2 < 6:
+                inter_s(c + 2, 0)
+            if 0 <= c < 6:
+                sig(c)
+            if 0 <= c + 2 < 6:
+                inter_v(c + 2)
+                inter_s(c + 2, 1)
+            if c == -2:
+                weights_turn(0, 0, 2)
+                weights_turn(0, 2, 1)
+            if 0 <= c < 6:
+                fixv(c)

@@ -20,6 +20,7 @@ NA = 3
 NO = 128
 Y_SCALE = 190.0
 MANUAL = False
+V_SHARE = [80, 64, 56, 56, 56]
 
 
 def tile_head_kernel(tc, f0, f1, f2, w0, b0, w1, b1, w2, b2, anchors, out_0, out_1):
@@ -39,12 +40,43 @@ def tile_head_kernel(tc, f0, f1, f2, w0, b0, w1, b1, w2, b2, anchors, out_0, out
         wr2 = keep.tile([P, NA, 1024], BF16, name="wr2")
         rawl1 = keep.tile([P, 2, 4, 256], BF16, name="rawl1")
         rawl2 = keep.tile([P, 2, 2, 4, 64], BF16, name="rawl2")
+        rows_a = keep.tile([P, 416], BF16, name="rows_a")
+        rows_b = keep.tile([P, 672], BF16, name="rows_b")
+        ones = keep.tile([P, P], BF16, name="ones")
+        halves = keep.tile([P, P], BF16, name="halves")
+        ident = keep.tile([P, P], F32, name="ident")
+        fg2 = keep.tile([P, 8, 64, 4], BF16, name="fg2", align_bytes=64)
+        fq2 = keep.tile([P, 576], U32, name="fq2", align_bytes=64)
+        fs2 = keep.tile([P, 576], U8, name="fs2", align_bytes=64)
+        warm = keep.tile([P, 2], F32, name="warm")
+
+        nc.gpsimd.memset(rows_a[:].bitcast(F32), 0.0)
+        nc.gpsimd.memset(ones[:], 1.0)
+        make_identity(nc, ident[:])
+        nc.gpsimd.memset(rows_b[:].bitcast(F32), 0.0)
+        nc.gpsimd.memset(halves[:], 0.0)
+        nc.gpsimd.memset(halves[0:64, 0:64], 1.0)
+        nc.gpsimd.memset(halves[64:128, 64:128], 1.0)
+        nc.gpsimd.memset(fg2[:].rearrange("p b x j -> p (b x j)").bitcast(F32), 0.0)
+        nc.vector.memset(warm[:], 0.0)
+        nc.vector.memset(fq2[:, 512:576].bitcast(I32), 0)
+        nc.vector.memset(fs2[:, 512:576].bitcast(I32), 0)
+        nc.scalar.activation(out=warm[:, 1:2], in_=warm[:, 0:1], func=ACT.Sigmoid)
+
         f0n0 = f0[0].rearrange("(p j) u v -> p j (u v)", j=4)
         f0n1 = f0[1].rearrange("(p j) u v -> p j (u v)", j=4)
-        nc.sync.dma_start(out=raw00[:], in_=f0n0[:, :, 0:512])
+        anc = anchors.rearrange("(o l) a w -> o (l a w)", o=1)
         nc.sync.dma_start(out=wr0[:], in_=w0.rearrange("(a r) k -> r a k", a=NA))
+        nc.sync.dma_start(out=rows_a[0:1, 0:384], in_=b0.rearrange("(o c) -> o c", o=1))
+        nc.sync.dma_start(out=rows_a[0:1, 384:396], in_=anc[:, 0:12])
+        nc.sync.dma_start(out=raw00[:], in_=f0n0[:, :, 0:512])
         nc.sync.dma_start(out=raw01[:], in_=f0n0[:, :, 512:1024])
         nc.sync.dma_start(out=raw1x[:], in_=f0n1)
+        nc.sync.dma_start(out=rows_b[0:1, 0:384], in_=b1.rearrange("(o c) -> o c", o=1))
+        nc.sync.dma_start(out=rows_b[0:1, 384:640], in_=b2[0:256].rearrange("(o c) -> o c", o=1))
+        nc.sync.dma_start(out=rows_b[64:65, 384:640], in_=b2[128:384].rearrange("(o c) -> o c", o=1))
+        nc.sync.dma_start(out=rows_b[0:1, 640:644], in_=anc[:, 12:16])
+        nc.sync.dma_start(out=rows_b[64:65, 640:644], in_=anc[:, 14:18])
         nc.sync.dma_start(out=wr1[:], in_=w1.rearrange("(a r) k -> r a k", a=NA))
         nc.sync.dma_start(
             out=rawl1[:].rearrange("p n j x -> p n (j x)"),
@@ -57,59 +89,37 @@ def tile_head_kernel(tc, f0, f1, f2, w0, b0, w1, b1, w2, b2, anchors, out_0, out
                 in_=f2[n].rearrange("(k p j) u v -> p k (j u v)", k=2, j=4),
             )
 
-        rows = keep.tile([P, 1056], BF16, name="rows")
-        nc.vector.memset(rows[:].bitcast(I32), 0)
-        warm = keep.tile([P, 2], F32, name="warm")
-        nc.vector.memset(warm[:], 0.0)
-        anc = anchors.rearrange("(o l) a w -> o (l a w)", o=1)
-        nc.scalar.dma_start(out=rows[0:1, 0:384], in_=b0.rearrange("(o c) -> o c", o=1))
-        nc.scalar.dma_start(out=rows[0:1, 1024:1042], in_=anc)
-        nc.scalar.dma_start(out=rows[0:1, 384:768], in_=b1.rearrange("(o c) -> o c", o=1))
-        nc.scalar.dma_start(out=rows[0:1, 768:1024], in_=b2[0:256].rearrange("(o c) -> o c", o=1))
-        nc.scalar.dma_start(out=rows[64:65, 768:1024], in_=b2[128:384].rearrange("(o c) -> o c", o=1))
-        nc.scalar.dma_start(out=rows[64:65, 1036:1040], in_=anc[:, 14:18])
-        nc.scalar.activation(out=warm[:, 1:2], in_=warm[:, 0:1], func=ACT.Sigmoid)
-
-        ones = keep.tile([P, P], BF16, name="ones")
-        halves = keep.tile([P, P], BF16, name="halves")
-        ident = keep.tile([P, P], F32, name="ident")
-        nc.gpsimd.memset(ones[:], 1.0)
-        nc.gpsimd.memset(halves[:], 0.0)
-        nc.gpsimd.memset(halves[0:64, 0:64], 1.0)
-        nc.gpsimd.memset(halves[64:128, 64:128], 1.0)
-        make_identity(nc, ident[:])
-
-        fg2 = keep.tile([P, 8, 64, 4], BF16, name="fg2", align_bytes=64)
-        nc.gpsimd.memset(fg2[:], 0.0)
-        fq2 = keep.tile([P, 576], U32, name="fq2", align_bytes=64)
-        fs2 = keep.tile([P, 576], U8, name="fs2", align_bytes=64)
-        nc.vector.memset(fq2[:, 512:576].bitcast(I32), 0)
-        nc.vector.memset(fs2[:, 512:576].bitcast(I32), 0)
-
-        pb = ps_xt.tile([P, 1024], BF16, tag="xt")
-        nc.tensor.matmul(out=pb[:, 0:384], lhsT=ones[:], rhs=rows[:, 0:384], start=True, stop=True)
-        nc.tensor.matmul(out=pb[:, 384:768], lhsT=ones[:], rhs=rows[:, 384:768], start=True, stop=True)
-        nc.tensor.matmul(out=pb[:, 768:1024], lhsT=halves[:], rhs=rows[:, 768:1024], start=True, stop=True)
-        pa = ps_xt.tile([P, 16], F32, tag="xt")
-        nc.tensor.matmul(out=pa[:, 0:12], lhsT=ones[:], rhs=rows[:, 1024:1036], start=True, stop=True)
-        nc.tensor.matmul(out=pa[:, 12:16], lhsT=halves[:], rhs=rows[:, 1036:1040], start=True, stop=True)
         bias = keep.tile([P, 1024], BF16, name="bias")
-        nc.scalar.copy(out=bias[:], in_=pb[:])
         a4 = keep.tile([P, 2, NA, 4, 2], F32, name="a4")
-        for lv in range(2):
-            nc.scalar.activation(
-                out=a4[:, lv],
-                in_=pa[:, 6 * lv : 6 * lv + 6]
-                .rearrange("p (a w) -> p a w", w=2)
-                .unsqueeze(2)
-                .to_broadcast([P, NA, 4, 2]),
-                func=ACT.Copy,
-                scale=4.0,
-            )
         a42 = keep.tile([P, 2, 4], F32, name="a42")
-        nc.scalar.activation(
-            out=a42[:], in_=pa[:, 12:16].unsqueeze(1).to_broadcast([P, 2, 4]), func=ACT.Copy, scale=4.0
-        )
+
+        def spread_a():
+            pb = ps_xt.tile([P, 384], BF16, tag="xt")
+            nc.tensor.matmul(out=pb[:], lhsT=ones[:], rhs=rows_a[:, 0:384], start=True, stop=True)
+            pa = ps_xt.tile([P, 12], F32, tag="xt")
+            nc.tensor.matmul(out=pa[:], lhsT=ones[:], rhs=rows_a[:, 384:396], start=True, stop=True)
+            nc.scalar.copy(out=bias[:, 0:384], in_=pb[:])
+            for lv in range(2):
+                nc.scalar.activation(
+                    out=a4[:, lv],
+                    in_=pa[:, 6 * lv : 6 * lv + 6]
+                    .rearrange("p (a w) -> p a w", w=2)
+                    .unsqueeze(2)
+                    .to_broadcast([P, NA, 4, 2]),
+                    func=ACT.Copy,
+                    scale=4.0,
+                )
+
+        def spread_b():
+            pb = ps_xt.tile([P, 640], BF16, tag="xt")
+            nc.tensor.matmul(out=pb[:, 0:384], lhsT=ones[:], rhs=rows_b[:, 0:384], start=True, stop=True)
+            nc.tensor.matmul(out=pb[:, 384:640], lhsT=halves[:], rhs=rows_b[:, 384:640], start=True, stop=True)
+            pa = ps_xt.tile([P, 4], F32, tag="xt")
+            nc.tensor.matmul(out=pa[:], lhsT=halves[:], rhs=rows_b[:, 640:644], start=True, stop=True)
+            nc.scalar.copy(out=bias[:, 384:1024], in_=pb[:])
+            nc.scalar.activation(
+                out=a42[:], in_=pa[:].unsqueeze(1).to_broadcast([P, 2, 4]), func=ACT.Copy, scale=4.0
+            )
 
         wraws = [wr0, wr1, wr2]
         wq = []
@@ -170,40 +180,42 @@ def tile_head_kernel(tc, f0, f1, f2, w0, b0, w1, b1, w2, b2, anchors, out_0, out
         ot.append(o2)
         qt.append(q2)
 
-        def pieces(c):
+        def piece(c, m0, m1):
             if c < 4:
                 src = [raw00[:], raw01[:], raw1x[:, :, 0:512], raw1x[:, :, 512:1024]][c]
-                sv = src.rearrange("p j (m g) -> p g m j", g=4)
-                return [(fg[c][:, g : g + 1], sv[:, g : g + 1]) for g in range(4)]
-            if c == 4:
-                res = []
-                for n in range(2):
-                    sv = rawl1[:, n].rearrange("p j (m g) -> p g m j", g=2)
-                    for g in range(2):
-                        res.append((fg[c][:, 2 * n + g : 2 * n + g + 1], sv[:, g : g + 1]))
-                return res
+                return [
+                    (
+                        fg[c][:, :, m0:m1, :].rearrange("p g m j -> p m g j"),
+                        src[:, :, 4 * m0 : 4 * m1].rearrange("p j (m g) -> p m g j", g=4),
+                    )
+                ]
+            return [
+                (
+                    fg[c][:, 2 * n : 2 * n + 2, m0:m1, :].rearrange("p g m j -> p m g j"),
+                    rawl1[:, n, :, 2 * m0 : 2 * m1].rearrange("p j (m g) -> p m g j", g=2),
+                )
+                for n in range(2)
+            ]
+
+        def piece2(q0, q1):
             dst = fg2[:].rearrange("p (q z) x j -> p q z x j", z=2)[:, :, 1]
             sv = rawl2[:].rearrange("p n k j x -> p (n k) x j")
-            return [(dst[:, 0:2], sv[:, 0:2]), (dst[:, 2:4], sv[:, 2:4])]
+            return [(dst[:, q0:q1], sv[:, q0:q1])]
 
         def inter_v(c):
-            pc = pieces(c)
-            if c < 4:
-                src = [raw00[:], raw01[:], raw1x[:, :, 0:512], raw1x[:, :, 512:1024]][c]
-                sv = src.rearrange("p j (m g) -> p g m j", g=4)
-                nc.vector.tensor_copy(out=fg[c][:, 0:2], in_=sv[:, 0:2])
-            elif c == 4:
-                sv = rawl1[:, 0].rearrange("p j (m g) -> p g m j", g=2)
-                nc.vector.tensor_copy(out=fg[c][:, 0:2], in_=sv)
-            else:
-                nc.vector.tensor_copy(out=pc[0][0], in_=pc[0][1])
+            todo = piece(c, 0, V_SHARE[c]) if c < 5 else piece2(0, 2)
+            for o_ap, i_ap in todo:
+                nc.vector.tensor_copy(out=o_ap, in_=i_ap)
 
         def inter_s(c, part):
-            pc = pieces(c)
             if c < 5:
-                nc.scalar.copy(out=pc[2 + part][0], in_=pc[2 + part][1])
-            elif part == 0:
-                nc.scalar.copy(out=pc[1][0], in_=pc[1][1])
+                mid = (V_SHARE[c] + P) // 2
+                mid = mid - mid % 4
+                todo = piece(c, V_SHARE[c], mid) if part == 0 else piece(c, mid, P)
+            else:
+                todo = piece2(2, 4) if part == 0 else []
+            for o_ap, i_ap in todo:
+                nc.scalar.copy(out=o_ap, in_=i_ap)
 
         def quant(c):
             if c < 5:
@@ -347,26 +359,30 @@ def tile_head_kernel(tc, f0, f1, f2, w0, b0, w1, b1, w2, b2, anchors, out_0, out
             for i in range(len(ds)):
                 nc.sync.dma_start(out=ds[i], in_=ss[i])
 
+        weights_turn(0, 0, 2)
+        weights_turn(0, 2, 1)
+        weights_quant(0, 0, 2)
+        weights_quant(0, 2, 1)
+        spread_a()
         for c in range(-2, 7):
             if 0 <= c + 1 < 6:
                 quant(c + 1)
-            if c == -1:
-                weights_quant(0, 0, 2)
-                weights_quant(0, 2, 1)
-            if 0 <= c + 1 < 6:
                 mm(c + 1)
-            if 0 <= c - 1 < 6:
+            if 0 <= c - 1 < 4:
                 store0(c - 1)
-                for part in range(3 if c - 1 < 5 else 1):
+                for part in range(3):
                     cast(c - 1, part)
                 store1(c - 1)
             if c == 1:
+                spread_b()
                 weights_turn(1, 0, 2)
                 weights_turn(1, 2, 1)
             if c == 2:
                 weights_turn(2, 0, 2)
                 weights_turn(2, 2, 2)
                 weights_turn(2, 4, 2)
+            if c == 5:
+                store0(4)
             if 0 <= c < 6:
                 badd(c)
             if c == 1:
@@ -375,6 +391,8 @@ def tile_head_kernel(tc, f0, f1, f2, w0, b0, w1, b1, w2, b2, anchors, out_0, out
             if c == 2:
                 weights_quant(2, 0, 4)
                 weights_quant(2, 4, 2)
+            if c == 5:
+                cast(4, 0)
             if 0 <= c + 2 < 6:
                 inter_s(c + 2, 0)
             if 0 <= c < 6:
@@ -382,8 +400,13 @@ def tile_head_kernel(tc, f0, f1, f2, w0, b0, w1, b1, w2, b2, anchors, out_0, out
             if 0 <= c + 2 < 6:
                 inter_v(c + 2)
                 inter_s(c + 2, 1)
-            if c == -2:
-                weights_turn(0, 0, 2)
-                weights_turn(0, 2, 1)
+            if c == 5:
+                cast(4, 2, on_vector=True)
+                cast(4, 1)
+                store1(4)
             if 0 <= c < 6:
                 fixv(c)
+            if c == 6:
+                store0(5)
+                cast(5, 0, on_vector=True)
+                store1(5)

@@ -19,8 +19,9 @@ P = 128
 NA = 3
 NO = 128
 Y_SCALE = 190.0
-MANUAL = False
-V_SHARE = [80, 64, 56, 56, 56]
+MANUAL = True
+V_SHARE = [64, 72, 48, 48]
+V_CASTS = [(4, 1), (4, 2)]
 
 
 def tile_head_kernel(tc, f0, f1, f2, w0, b0, w1, b1, w2, b2, anchors, out_0, out_1):
@@ -32,7 +33,8 @@ def tile_head_kernel(tc, f0, f1, f2, w0, b0, w1, b1, w2, b2, anchors, out_0, out
         if MANUAL:
             ctx.enter_context(tc.manual_schedule())
 
-        raw00 = keep.tile([P, 4, 512], BF16, name="raw00")
+        raw00a = keep.tile([P, 4, 256], BF16, name="raw00a")
+        raw00b = keep.tile([P, 4, 256], BF16, name="raw00b")
         raw01 = keep.tile([P, 4, 512], BF16, name="raw01")
         raw1x = keep.tile([P, 4, 1024], BF16, name="raw1x")
         wr0 = keep.tile([P, NA, 512], BF16, name="wr0")
@@ -51,8 +53,8 @@ def tile_head_kernel(tc, f0, f1, f2, w0, b0, w1, b1, w2, b2, anchors, out_0, out
         warm = keep.tile([P, 2], F32, name="warm")
 
         nc.gpsimd.memset(rows_a[:].bitcast(F32), 0.0)
-        nc.gpsimd.memset(ones[:], 1.0)
         make_identity(nc, ident[:])
+        nc.gpsimd.memset(ones[:], 1.0)
         nc.gpsimd.memset(rows_b[:].bitcast(F32), 0.0)
         nc.gpsimd.memset(halves[:], 0.0)
         nc.gpsimd.memset(halves[0:64, 0:64], 1.0)
@@ -66,60 +68,74 @@ def tile_head_kernel(tc, f0, f1, f2, w0, b0, w1, b1, w2, b2, anchors, out_0, out
         f0n0 = f0[0].rearrange("(p j) u v -> p j (u v)", j=4)
         f0n1 = f0[1].rearrange("(p j) u v -> p j (u v)", j=4)
         anc = anchors.rearrange("(o l) a w -> o (l a w)", o=1)
-        nc.sync.dma_start(out=wr0[:], in_=w0.rearrange("(a r) k -> r a k", a=NA))
-        nc.sync.dma_start(out=rows_a[0:1, 0:384], in_=b0.rearrange("(o c) -> o c", o=1))
-        nc.sync.dma_start(out=rows_a[0:1, 384:396], in_=anc[:, 0:12])
-        nc.sync.dma_start(out=raw00[:], in_=f0n0[:, :, 0:512])
-        nc.sync.dma_start(out=raw01[:], in_=f0n0[:, :, 512:1024])
-        nc.sync.dma_start(out=raw1x[:], in_=f0n1)
-        nc.sync.dma_start(out=rows_b[0:1, 0:384], in_=b1.rearrange("(o c) -> o c", o=1))
-        nc.sync.dma_start(out=rows_b[0:1, 384:640], in_=b2[0:256].rearrange("(o c) -> o c", o=1))
-        nc.sync.dma_start(out=rows_b[64:65, 384:640], in_=b2[128:384].rearrange("(o c) -> o c", o=1))
-        nc.sync.dma_start(out=rows_b[0:1, 640:644], in_=anc[:, 12:16])
-        nc.sync.dma_start(out=rows_b[64:65, 640:644], in_=anc[:, 14:18])
-        nc.sync.dma_start(out=wr1[:], in_=w1.rearrange("(a r) k -> r a k", a=NA))
-        nc.sync.dma_start(
-            out=rawl1[:].rearrange("p n j x -> p n (j x)"),
-            in_=f1.rearrange("n (p j) u v -> p n (j u v)", j=4),
-        )
-        nc.sync.dma_start(out=wr2[:], in_=w2.rearrange("(a r) k -> r a k", a=NA))
-        for n in range(2):
+        w0v = w0.rearrange("(a r) k -> r a k", a=NA)
+        if True:
+            nc.sync.dma_start(out=wr0[:, 0:2], in_=w0v[:, 0:2])
+            nc.sync.dma_start(out=raw00a[:], in_=f0n0[:, :, 0:256])
+            nc.sync.dma_start(out=rows_a[0:1, 0:384], in_=b0.rearrange("(o c) -> o c", o=1))
+            nc.sync.dma_start(out=rows_a[0:1, 384:396], in_=anc[:, 0:12])
+            nc.sync.dma_start(out=wr0[:, 2:3], in_=w0v[:, 2:3])
+            nc.sync.dma_start(out=raw00b[:], in_=f0n0[:, :, 256:512])
+            nc.sync.dma_start(out=raw01[:], in_=f0n0[:, :, 512:1024])
+            nc.sync.dma_start(out=rows_b[0:1, 0:384], in_=b1.rearrange("(o c) -> o c", o=1))
+            nc.sync.dma_start(out=rows_b[0:1, 384:640], in_=b2[0:256].rearrange("(o c) -> o c", o=1))
+            nc.sync.dma_start(out=rows_b[64:65, 384:640], in_=b2[128:384].rearrange("(o c) -> o c", o=1))
+            nc.sync.dma_start(out=rows_b[0:1, 640:644], in_=anc[:, 12:16])
+            nc.sync.dma_start(out=rows_b[64:65, 640:644], in_=anc[:, 14:18])
+            nc.sync.dma_start(out=raw1x[:], in_=f0n1)
+            nc.sync.dma_start(out=wr2[:], in_=w2.rearrange("(a r) k -> r a k", a=NA))
+            for n in range(2):
+                nc.sync.dma_start(
+                    out=rawl2[:, n].rearrange("p k j x -> p k (j x)"),
+                    in_=f2[n].rearrange("(k p j) u v -> p k (j u v)", k=2, j=4),
+                )
+            nc.sync.dma_start(out=wr1[:], in_=w1.rearrange("(a r) k -> r a k", a=NA))
             nc.sync.dma_start(
-                out=rawl2[:, n].rearrange("p k j x -> p k (j x)"),
-                in_=f2[n].rearrange("(k p j) u v -> p k (j u v)", k=2, j=4),
+                out=rawl1[:].rearrange("p n j x -> p n (j x)"),
+                in_=f1.rearrange("n (p j) u v -> p n (j u v)", j=4),
             )
 
         bias = keep.tile([P, 1024], BF16, name="bias")
-        a4 = keep.tile([P, 2, NA, 4, 2], F32, name="a4")
-        a42 = keep.tile([P, 2, 4], F32, name="a42")
+        a4x = keep.tile([P, 14, 2], F32, name="a4x")
+        a4y = keep.tile([P, 14, 2], F32, name="a4y")
 
-        def spread_a():
+        def times4(dst, src):
+            nc.scalar.activation(out=dst, in_=src, func=ACT.Copy, scale=4.0)
+
+        held = {}
+
+        def spread_a_pe():
             pb = ps_xt.tile([P, 384], BF16, tag="xt")
             nc.tensor.matmul(out=pb[:], lhsT=ones[:], rhs=rows_a[:, 0:384], start=True, stop=True)
             pa = ps_xt.tile([P, 12], F32, tag="xt")
             nc.tensor.matmul(out=pa[:], lhsT=ones[:], rhs=rows_a[:, 384:396], start=True, stop=True)
-            nc.scalar.copy(out=bias[:, 0:384], in_=pb[:])
-            for lv in range(2):
-                nc.scalar.activation(
-                    out=a4[:, lv],
-                    in_=pa[:, 6 * lv : 6 * lv + 6]
-                    .rearrange("p (a w) -> p a w", w=2)
-                    .unsqueeze(2)
-                    .to_broadcast([P, NA, 4, 2]),
-                    func=ACT.Copy,
-                    scale=4.0,
-                )
+            held["pb_a"] = pb
+            held["pa_a"] = pa
 
-        def spread_b():
+        def spread_a_s():
+            pb = held["pb_a"]
+            pa = held["pa_a"]
+            nc.scalar.copy(out=bias[:, 0:384], in_=pb[:])
+            lv0 = pa[:, 0:6].rearrange("p (a w) -> p a w", w=2).unsqueeze(2).to_broadcast([P, NA, 4, 2])
+            lv1 = pa[:, 6:12].rearrange("p (a w) -> p a w", w=2).unsqueeze(2).to_broadcast([P, NA, 4, 2])
+            times4(a4x[:, 0:12, :].rearrange("p (a g) w -> p a g w", g=4), lv0)
+            times4(a4y[:, 0:12, :].rearrange("p (a g) w -> p a g w", g=4), lv1)
+
+        def spread_b_pe():
             pb = ps_xt.tile([P, 640], BF16, tag="xt")
             nc.tensor.matmul(out=pb[:, 0:384], lhsT=ones[:], rhs=rows_b[:, 0:384], start=True, stop=True)
             nc.tensor.matmul(out=pb[:, 384:640], lhsT=halves[:], rhs=rows_b[:, 384:640], start=True, stop=True)
             pa = ps_xt.tile([P, 4], F32, tag="xt")
             nc.tensor.matmul(out=pa[:], lhsT=halves[:], rhs=rows_b[:, 640:644], start=True, stop=True)
+            held["pb_b"] = pb
+            held["pa_b"] = pa
+
+        def spread_b_s():
+            pb = held["pb_b"]
+            pa = held["pa_b"]
             nc.scalar.copy(out=bias[:, 384:1024], in_=pb[:])
-            nc.scalar.activation(
-                out=a42[:], in_=pa[:].unsqueeze(1).to_broadcast([P, 2, 4]), func=ACT.Copy, scale=4.0
-            )
+            times4(a4x[:, 12:14, :], pa[:, 0:2].unsqueeze(1).to_broadcast([P, 2, 2]))
+            times4(a4y[:, 12:14, :], pa[:, 2:4].unsqueeze(1).to_broadcast([P, 2, 2]))
 
         wraws = [wr0, wr1, wr2]
         wq = []
@@ -134,7 +150,7 @@ def tile_head_kernel(tc, f0, f1, f2, w0, b0, w1, b1, w2, b2, anchors, out_0, out
             wq.append(wq_t)
             ws.append(ws_t)
 
-        def weights_turn(lv, q0, nq):
+        def turn_pe(lv, q0, nq):
             words = wraws[lv][:].bitcast(F32)
             xt = ps_xt.tile([P, 2, 2, NO], F32, tag="xt")
             for i in range(nq):
@@ -143,6 +159,10 @@ def tile_head_kernel(tc, f0, f1, f2, w0, b0, w1, b1, w2, b2, anchors, out_0, out
                     nc.tensor.transpose(
                         xt[:, i, u, :], words[:, a, 256 * kp + u : 256 * (kp + 1) : 2], ident[:]
                     )
+            held[(lv, q0)] = xt
+
+        def turn_s(lv, q0, nq):
+            xt = held[(lv, q0)]
             nc.scalar.copy(
                 out=wgs[lv][:].bitcast(F32)[:, q0 : q0 + nq],
                 in_=xt[:, 0:nq].rearrange("p i u r -> p i r u"),
@@ -159,62 +179,59 @@ def tile_head_kernel(tc, f0, f1, f2, w0, b0, w1, b1, w2, b2, anchors, out_0, out
         fg = []
         fq = []
         fs = []
-        ot = []
-        qt = []
         for c in range(5):
             fg_t = keep.tile([P, 4, P, 4], BF16, name="fg_%d" % c, align_bytes=64)
             fq_t = keep.tile([P, 512], U32, name="fq_%d" % c, align_bytes=64)
             fs_t = keep.tile([P, 512], U8, name="fs_%d" % c, align_bytes=64)
-            o_t = keep.tile([P, NA, 4, NO], F32, name="o_%d" % c)
-            q_t = keep.tile([P, NA * 4 * NO], FP8, name="q_%d" % c)
             fg.append(fg_t)
             fq.append(fq_t)
             fs.append(fs_t)
-            ot.append(o_t)
-            qt.append(q_t)
-        o2 = keep.tile([P, 4, NO], F32, name="o_5")
-        q2 = keep.tile([P, 4 * NO], FP8, name="q_5")
         fg.append(fg2)
         fq.append(fq2)
         fs.append(fs2)
-        ot.append(o2)
-        qt.append(q2)
+        n_rows = [12, 12, 12, 14, 14]
+        og = []
+        qg = []
+        for g in range(5):
+            o_t = keep.tile([P, n_rows[g], NO], F32, name="o_%d" % g)
+            q_t = keep.tile([P, n_rows[g] * NO], FP8, name="q_%d" % g)
+            og.append(o_t)
+            qg.append(q_t)
 
-        def piece(c, m0, m1):
-            if c < 4:
-                src = [raw00[:], raw01[:], raw1x[:, :, 0:512], raw1x[:, :, 512:1024]][c]
+        def walk(dst, src, g):
+            return (dst.rearrange("p g m j -> p m g j"), src.rearrange("p j (m g) -> p m g j", g=g))
+
+        def pieces(c):
+            if c == 0:
                 return [
-                    (
-                        fg[c][:, :, m0:m1, :].rearrange("p g m j -> p m g j"),
-                        src[:, :, 4 * m0 : 4 * m1].rearrange("p j (m g) -> p m g j", g=4),
-                    )
+                    walk(fg[0][:, :, 0:64, :], raw00a[:], 4),
+                    walk(fg[0][:, :, 64:128, :], raw00b[:], 4),
                 ]
-            return [
-                (
-                    fg[c][:, 2 * n : 2 * n + 2, m0:m1, :].rearrange("p g m j -> p m g j"),
-                    rawl1[:, n, :, 2 * m0 : 2 * m1].rearrange("p j (m g) -> p m g j", g=2),
-                )
-                for n in range(2)
-            ]
-
-        def piece2(q0, q1):
+            if c < 4:
+                src = [raw01[:], raw1x[:, :, 0:512], raw1x[:, :, 512:1024]][c - 1]
+                mv = V_SHARE[c]
+                mid = (mv + P) // 2
+                return [
+                    walk(fg[c][:, :, 0:mv, :], src[:, :, 0 : 4 * mv], 4),
+                    walk(fg[c][:, :, mv:mid, :], src[:, :, 4 * mv : 4 * mid], 4),
+                    walk(fg[c][:, :, mid:P, :], src[:, :, 4 * mid : 4 * P], 4),
+                ]
+            if c == 4:
+                return [
+                    walk(fg[4][:, 0:2], rawl1[:, 0], 2),
+                    walk(fg[4][:, 2:4, 0:64, :], rawl1[:, 1, :, 0:128], 2),
+                    walk(fg[4][:, 2:4, 64:128, :], rawl1[:, 1, :, 128:256], 2),
+                ]
             dst = fg2[:].rearrange("p (q z) x j -> p q z x j", z=2)[:, :, 1]
             sv = rawl2[:].rearrange("p n k j x -> p (n k) x j")
-            return [(dst[:, q0:q1], sv[:, q0:q1])]
+            return [(dst[:, 0:1], sv[:, 0:1]), (dst[:, 1:4], sv[:, 1:4])]
 
         def inter_v(c):
-            todo = piece(c, 0, V_SHARE[c]) if c < 5 else piece2(0, 2)
-            for o_ap, i_ap in todo:
-                nc.vector.tensor_copy(out=o_ap, in_=i_ap)
+            pc = pieces(c)
+            nc.vector.tensor_copy(out=pc[0][0], in_=pc[0][1])
 
-        def inter_s(c, part):
-            if c < 5:
-                mid = (V_SHARE[c] + P) // 2
-                mid = mid - mid % 4
-                todo = piece(c, V_SHARE[c], mid) if part == 0 else piece(c, mid, P)
-            else:
-                todo = piece2(2, 4) if part == 0 else []
-            for o_ap, i_ap in todo:
+        def inter_s(c):
+            for o_ap, i_ap in pieces(c)[1:]:
                 nc.scalar.copy(out=o_ap, in_=i_ap)
 
         def quant(c):
@@ -243,9 +260,9 @@ def tile_head_kernel(tc, f0, f1, f2, w0, b0, w1, b1, w2, b2, anchors, out_0, out
                         )
                     banks[(c, a)] = acc
             else:
-                acc = ps_mm.tile([P, 4, NO], F32, tag="acc")
-                for n in range(2):
-                    for t in range(2):
+                for t in range(2):
+                    acc = ps_mm.tile([P, 2, NO], F32, tag="acc")
+                    for n in range(2):
                         todo = []
                         for half in range(2):
                             for kp in range(2):
@@ -253,7 +270,7 @@ def tile_head_kernel(tc, f0, f1, f2, w0, b0, w1, b1, w2, b2, anchors, out_0, out
                         for i in range(4):
                             fc, wc = todo[i]
                             nc.tensor.matmul_mx(
-                                out=acc[:, 2 * n + t, :],
+                                out=acc[:, n, :],
                                 lhsT=fq2[:, fc : fc + P].bitcast(FP8X4),
                                 lhsT_scale=fs2[:, fc : fc + P],
                                 rhs=wq[2][:, wc : wc + NO].bitcast(FP8X4),
@@ -261,152 +278,138 @@ def tile_head_kernel(tc, f0, f1, f2, w0, b0, w1, b1, w2, b2, anchors, out_0, out
                                 start=(i == 0),
                                 stop=(i == 3),
                             )
-                banks[(c, 0)] = acc
+                    banks[(c, t)] = acc
+
+        def add_bias(dst, acc, col, reps):
+            nc.vector.tensor_tensor(
+                out=dst,
+                in0=acc[:],
+                in1=bias[:, col : col + NO].unsqueeze(1).to_broadcast([P, reps, NO]),
+                op=ALU.add,
+            )
 
         def badd(c):
-            if c < 5:
-                off = 0 if c < 4 else 384
-                for a in range(NA):
-                    nc.vector.tensor_tensor(
-                        out=ot[c][:, a],
-                        in0=banks[(c, a)][:],
-                        in1=bias[:, off + a * NO : off + (a + 1) * NO].unsqueeze(1).to_broadcast([P, 4, NO]),
-                        op=ALU.add,
-                    )
-            else:
-                nc.vector.tensor_tensor(
-                    out=o2[:].rearrange("p (n t) j -> p n (t j)", n=2),
-                    in0=banks[(c, 0)][:].rearrange("p (n t) j -> p n (t j)", n=2),
-                    in1=bias[:, 768:1024].unsqueeze(1).to_broadcast([P, 2, 2 * NO]),
-                    op=ALU.add,
-                )
+            for a in range(NA):
+                add_bias(og[c][:, 4 * a : 4 * a + 4, :], banks[(c, a)], (0 if c < 4 else 384) + a * NO, 4)
+            if c >= 3:
+                add_bias(og[c][:, 12:14, :], banks[(5, c - 3)], 768 + NO * (c - 3), 2)
 
         sgs = {}
 
-        def rows_of(c):
-            if c < 5:
-                return ot[c][:].rearrange("p a s j -> p (a s) j")
-            return o2[:]
+        def sig(g):
+            sg = keep.tile([P, n_rows[g], 4], F32, name="sg%d" % g)
+            nc.scalar.activation(out=sg[:], in_=og[g][:, :, 0:4], func=ACT.Sigmoid)
+            sgs[g] = sg
 
-        def sig(c):
-            nr = 12 if c < 5 else 4
-            sg = keep.tile([P, nr, 4], F32, name="sg%d" % c)
-            nc.scalar.activation(out=sg[:], in_=rows_of(c)[:, :, 0:4], func=ACT.Sigmoid)
-            sgs[c] = sg
-
-        def fixv(c):
-            nr = 12 if c < 5 else 4
-            sg = sgs[c]
-            rv = rows_of(c)
-            if c < 5:
-                av = a4[:, 0 if c < 4 else 1].rearrange("p a g w -> p (a g) w")
-            else:
-                av = a42[:].rearrange("p n (t w) -> p (n t) w", w=2)
-            sa = keep.tile([P, nr, 2], F32, name="sa%d" % c)
+        def fixv(g):
+            sg = sgs[g]
+            rv = og[g]
+            av = a4y[:] if g == 4 else a4x[:, 0 : n_rows[g], :]
+            sa = keep.tile([P, n_rows[g], 2], F32, name="sa%d" % g)
             nc.vector.tensor_tensor(out=sa[:], in0=sg[:, :, 2:4], in1=av, op=ALU.mult)
             nc.vector.tensor_scalar(
                 out=rv[:, :, 0:2], in0=sg[:, :, 0:2], scalar1=2.0, scalar2=-0.5, op0=ALU.mult, op1=ALU.add
             )
             nc.vector.tensor_tensor(out=rv[:, :, 2:4], in0=sa[:], in1=sg[:, :, 2:4], op=ALU.mult)
 
-        def cast(c, part, on_vector=False):
-            if c < 5:
-                src = ot[c][:].rearrange("p a s j -> p (a s j)")[:, part * 512 : (part + 1) * 512]
-                dst = qt[c][:, part * 512 : (part + 1) * 512]
-            else:
-                src = o2[:].rearrange("p t j -> p (t j)")
-                dst = q2[:]
-            if on_vector:
+        cuts = [[0, 4, 8, 12], [0, 4, 8, 12], [0, 4, 8, 12], [0, 4, 8, 14], [0, 4, 8, 14]]
+
+        def cast(g, piece):
+            c0 = cuts[g][piece] * NO
+            c1 = cuts[g][piece + 1] * NO
+            src = og[g][:].rearrange("p r j -> p (r j)")[:, c0:c1]
+            dst = qg[g][:, c0:c1]
+            if (g, piece) in V_CASTS:
                 nc.vector.tensor_scalar(
                     out=dst, in0=src, scalar1=Y_SCALE, scalar2=None, op0=ALU.mult, saturate=False
                 )
             else:
                 nc.scalar.activation(out=dst, in_=src, func=ACT.Copy, scale=Y_SCALE, saturate=False)
 
-        def dests(c, out):
-            if c < 4:
-                n, h = divmod(c, 2)
+        def stores(g, out, flat):
+            if g < 4:
+                n, h = divmod(g, 2)
                 v = out[n, 0:3072, :].rearrange("(a h m g) j -> h m a (g j)", a=NA, h=2, m=P, g=4)
-                return [v[h]]
-            if c == 4:
-                return [
-                    out[n, 3072:3840, :].rearrange("(a m g) j -> m a (g j)", a=NA, m=P, g=2) for n in range(2)
-                ]
-            return [out[:, 3840 + 64 * t : 3968 + 64 * t, :].rearrange("n m j -> m n j") for t in range(2)]
-
-        def sources(c, tile_ap):
-            if c < 4:
-                return [tile_ap.rearrange("p (a x) -> p a x", a=NA)]
-            if c == 4:
-                v = tile_ap.rearrange("p (a n x) -> p n a x", a=NA, n=2)
-                return [v[:, n] for n in range(2)]
-            v = tile_ap.rearrange("p (n t j) -> p t n j", n=2, t=2)
-            return [v[:, t] for t in range(2)]
-
-        def store0(c):
-            if c < 5:
-                flat = ot[c][:].rearrange("p a s j -> p (a s j)")
+                nc.sync.dma_start(out=v[h], in_=flat[:, 0 : 12 * NO].rearrange("p (a x) -> p a x", a=NA))
             else:
-                flat = o2[:].rearrange("p t j -> p (t j)")
-            ds = dests(c, out_0)
-            ss = sources(c, flat)
-            for i in range(len(ds)):
-                nc.sync.dma_start(out=ds[i], in_=ss[i])
+                s = flat[:, 0 : 12 * NO].rearrange("p (a n x) -> p n a x", a=NA, n=2)
+                for n in range(2):
+                    nc.sync.dma_start(
+                        out=out[n, 3072:3840, :].rearrange("(a m g) j -> m a (g j)", a=NA, m=P, g=2),
+                        in_=s[:, n],
+                    )
+            if g >= 3:
+                r0 = 3840 + 64 * (g - 3)
+                nc.sync.dma_start(
+                    out=out[:, r0 : r0 + P, :].rearrange("n m j -> m n j"),
+                    in_=flat[:, 12 * NO : 14 * NO].rearrange("p (n j) -> p n j", n=2),
+                )
 
-        def store1(c):
-            ds = dests(c, out_1)
-            ss = sources(c, qt[c][:].bitcast(U8))
-            for i in range(len(ds)):
-                nc.sync.dma_start(out=ds[i], in_=ss[i])
+        def store0(g):
+            stores(g, out_0, og[g][:].rearrange("p r j -> p (r j)"))
 
-        weights_turn(0, 0, 2)
-        weights_turn(0, 2, 1)
+        def store1(g):
+            stores(g, out_1, qg[g][:].bitcast(U8))
+
+        def casts(g):
+            for piece in range(len(cuts[g]) - 1):
+                cast(g, piece)
+
+        turn_pe(0, 0, 2)
+        turn_pe(0, 2, 1)
+        turn_s(0, 0, 2)
+        inter_v(0)
+        inter_s(0)
+        turn_s(0, 2, 1)
         weights_quant(0, 0, 2)
         weights_quant(0, 2, 1)
-        spread_a()
-        for c in range(-2, 7):
-            if 0 <= c + 1 < 6:
+        spread_a_pe()
+        spread_a_s()
+        for c in range(-1, 6):
+            if c == -1:
+                spread_b_pe()
+            if c == 1:
+                turn_pe(2, 0, 2)
+                turn_pe(2, 2, 2)
+            if c == 2:
+                turn_pe(2, 4, 2)
+                turn_pe(1, 0, 2)
+            if c + 2 < 5:
+                inter_s(c + 2)
+            if c == -1:
+                spread_b_s()
+            if c == 1:
+                inter_s(5)
+                turn_s(2, 0, 2)
+                turn_s(2, 2, 2)
+            if c == 2:
+                turn_s(2, 4, 2)
+                turn_s(1, 0, 2)
+                turn_pe(1, 2, 1)
+                turn_s(1, 2, 1)
+            if c in (3, 4):
+                casts(c - 1)
+                store1(c - 1)
+            if 0 <= c < 5:
+                badd(c)
+            if c + 1 < 5:
                 quant(c + 1)
                 mm(c + 1)
-            if 0 <= c - 1 < 4:
-                store0(c - 1)
-                for part in range(3):
-                    cast(c - 1, part)
-                store1(c - 1)
             if c == 1:
-                spread_b()
-                weights_turn(1, 0, 2)
-                weights_turn(1, 2, 1)
-            if c == 2:
-                weights_turn(2, 0, 2)
-                weights_turn(2, 2, 2)
-                weights_turn(2, 4, 2)
-            if c == 5:
-                store0(4)
-            if 0 <= c < 6:
-                badd(c)
-            if c == 1:
-                weights_quant(1, 0, 2)
-                weights_quant(1, 2, 1)
+                inter_v(5)
             if c == 2:
                 weights_quant(2, 0, 4)
                 weights_quant(2, 4, 2)
-            if c == 5:
-                cast(4, 0)
-            if 0 <= c + 2 < 6:
-                inter_s(c + 2, 0)
-            if 0 <= c < 6:
-                sig(c)
-            if 0 <= c + 2 < 6:
+                quant(5)
+                mm(5)
+                weights_quant(1, 0, 2)
+                weights_quant(1, 2, 1)
+            if c + 2 < 5:
                 inter_v(c + 2)
-                inter_s(c + 2, 1)
-            if c == 5:
-                cast(4, 2, on_vector=True)
-                cast(4, 1)
-                store1(4)
-            if 0 <= c < 6:
+            if 0 <= c < 5:
+                sig(c)
                 fixv(c)
-            if c == 6:
-                store0(5)
-                cast(5, 0, on_vector=True)
-                store1(5)
+                store0(c)
+            if c in (1, 2, 5):
+                casts(c - 1)
+                store1(c - 1)

@@ -20,6 +20,7 @@ NA = 3
 NO = 128
 Y_SCALE = 190.0
 MANUAL = True
+N_WARM = 16
 V_SHARE = [64, 72, 48, 48]
 V_CASTS = [(4, 1), (4, 2)]
 
@@ -53,8 +54,8 @@ def tile_head_kernel(tc, f0, f1, f2, w0, b0, w1, b1, w2, b2, anchors, out_0, out
         warm = keep.tile([P, 2], F32, name="warm")
 
         nc.gpsimd.memset(rows_a[:].bitcast(F32), 0.0)
-        make_identity(nc, ident[:])
         nc.gpsimd.memset(ones[:], 1.0)
+        make_identity(nc, ident[:])
         nc.gpsimd.memset(rows_b[:].bitcast(F32), 0.0)
         nc.gpsimd.memset(halves[:], 0.0)
         nc.gpsimd.memset(halves[0:64, 0:64], 1.0)
@@ -218,9 +219,9 @@ def tile_head_kernel(tc, f0, f1, f2, w0, b0, w1, b1, w2, b2, anchors, out_0, out
                 ]
             if c == 4:
                 return [
-                    walk(fg[4][:, 0:2], rawl1[:, 0], 2),
-                    walk(fg[4][:, 2:4, 0:64, :], rawl1[:, 1, :, 0:128], 2),
-                    walk(fg[4][:, 2:4, 64:128, :], rawl1[:, 1, :, 128:256], 2),
+                    walk(fg[4][:, 0:2, 0:96, :], rawl1[:, 0, :, 0:192], 2),
+                    walk(fg[4][:, 2:4], rawl1[:, 1], 2),
+                    walk(fg[4][:, 0:2, 96:128, :], rawl1[:, 0, :, 192:256], 2),
                 ]
             dst = fg2[:].rearrange("p (q z) x j -> p q z x j", z=2)[:, :, 1]
             sv = rawl2[:].rearrange("p n k j x -> p (n k) x j")
@@ -355,6 +356,9 @@ def tile_head_kernel(tc, f0, f1, f2, w0, b0, w1, b1, w2, b2, anchors, out_0, out
             for piece in range(len(cuts[g]) - 1):
                 cast(g, piece)
 
+        pw = ps_xt.tile([P, P], F32, tag="xt")
+        for i in range(N_WARM):
+            nc.tensor.matmul(out=pw[:], lhsT=ones[:], rhs=ones[:], start=True, stop=True)
         turn_pe(0, 0, 2)
         turn_pe(0, 2, 1)
         turn_s(0, 0, 2)
@@ -387,6 +391,9 @@ def tile_head_kernel(tc, f0, f1, f2, w0, b0, w1, b1, w2, b2, anchors, out_0, out
                 turn_s(1, 0, 2)
                 turn_pe(1, 2, 1)
                 turn_s(1, 2, 1)
+            if c == 2:
+                casts(0)
+                store1(0)
             if c in (3, 4):
                 casts(c - 1)
                 store1(c - 1)
@@ -410,6 +417,6 @@ def tile_head_kernel(tc, f0, f1, f2, w0, b0, w1, b1, w2, b2, anchors, out_0, out
                 sig(c)
                 fixv(c)
                 store0(c)
-            if c in (1, 2, 5):
+            if c in (2, 5):
                 casts(c - 1)
                 store1(c - 1)

@@ -20,7 +20,6 @@ NA = 3
 NO = 128
 Y_SCALE = 190.0
 MANUAL = True
-N_WARM = 16
 V_SHARE = [64, 72, 48, 48]
 V_CASTS = [(4, 1), (4, 2)]
 
@@ -54,8 +53,8 @@ def tile_head_kernel(tc, f0, f1, f2, w0, b0, w1, b1, w2, b2, anchors, out_0, out
         warm = keep.tile([P, 2], F32, name="warm")
 
         nc.gpsimd.memset(rows_a[:].bitcast(F32), 0.0)
-        nc.gpsimd.memset(ones[:], 1.0)
         make_identity(nc, ident[:])
+        nc.gpsimd.memset(ones[:], 1.0)
         nc.gpsimd.memset(rows_b[:].bitcast(F32), 0.0)
         nc.gpsimd.memset(halves[:], 0.0)
         nc.gpsimd.memset(halves[0:64, 0:64], 1.0)
@@ -73,17 +72,17 @@ def tile_head_kernel(tc, f0, f1, f2, w0, b0, w1, b1, w2, b2, anchors, out_0, out
         if True:
             nc.sync.dma_start(out=wr0[:, 0:2], in_=w0v[:, 0:2])
             nc.sync.dma_start(out=raw00a[:], in_=f0n0[:, :, 0:256])
-            nc.sync.dma_start(out=rows_a[0:1, 0:384], in_=b0.rearrange("(o c) -> o c", o=1))
-            nc.sync.dma_start(out=rows_a[0:1, 384:396], in_=anc[:, 0:12])
             nc.sync.dma_start(out=wr0[:, 2:3], in_=w0v[:, 2:3])
             nc.sync.dma_start(out=raw00b[:], in_=f0n0[:, :, 256:512])
+            nc.sync.dma_start(out=rows_a[0:1, 0:384], in_=b0.rearrange("(o c) -> o c", o=1))
+            nc.sync.dma_start(out=rows_a[0:1, 384:396], in_=anc[:, 0:12])
             nc.sync.dma_start(out=raw01[:], in_=f0n0[:, :, 512:1024])
+            nc.sync.dma_start(out=raw1x[:], in_=f0n1)
             nc.sync.dma_start(out=rows_b[0:1, 0:384], in_=b1.rearrange("(o c) -> o c", o=1))
             nc.sync.dma_start(out=rows_b[0:1, 384:640], in_=b2[0:256].rearrange("(o c) -> o c", o=1))
             nc.sync.dma_start(out=rows_b[64:65, 384:640], in_=b2[128:384].rearrange("(o c) -> o c", o=1))
             nc.sync.dma_start(out=rows_b[0:1, 640:644], in_=anc[:, 12:16])
             nc.sync.dma_start(out=rows_b[64:65, 640:644], in_=anc[:, 14:18])
-            nc.sync.dma_start(out=raw1x[:], in_=f0n1)
             nc.sync.dma_start(out=wr2[:], in_=w2.rearrange("(a r) k -> r a k", a=NA))
             for n in range(2):
                 nc.sync.dma_start(
@@ -219,9 +218,9 @@ def tile_head_kernel(tc, f0, f1, f2, w0, b0, w1, b1, w2, b2, anchors, out_0, out
                 ]
             if c == 4:
                 return [
-                    walk(fg[4][:, 0:2, 0:96, :], rawl1[:, 0, :, 0:192], 2),
-                    walk(fg[4][:, 2:4], rawl1[:, 1], 2),
-                    walk(fg[4][:, 0:2, 96:128, :], rawl1[:, 0, :, 192:256], 2),
+                    walk(fg[4][:, 0:2], rawl1[:, 0], 2),
+                    walk(fg[4][:, 2:4, 0:64, :], rawl1[:, 1, :, 0:128], 2),
+                    walk(fg[4][:, 2:4, 64:128, :], rawl1[:, 1, :, 128:256], 2),
                 ]
             dst = fg2[:].rearrange("p (q z) x j -> p q z x j", z=2)[:, :, 1]
             sv = rawl2[:].rearrange("p n k j x -> p (n k) x j")
@@ -356,9 +355,6 @@ def tile_head_kernel(tc, f0, f1, f2, w0, b0, w1, b1, w2, b2, anchors, out_0, out
             for piece in range(len(cuts[g]) - 1):
                 cast(g, piece)
 
-        pw = ps_xt.tile([P, P], F32, tag="xt")
-        for i in range(N_WARM):
-            nc.tensor.matmul(out=pw[:], lhsT=ones[:], rhs=ones[:], start=True, stop=True)
         turn_pe(0, 0, 2)
         turn_pe(0, 2, 1)
         turn_s(0, 0, 2)
@@ -370,7 +366,7 @@ def tile_head_kernel(tc, f0, f1, f2, w0, b0, w1, b1, w2, b2, anchors, out_0, out
         spread_a_pe()
         spread_a_s()
         for c in range(-1, 6):
-            if c == -1:
+            if c == 0:
                 spread_b_pe()
             if c == 1:
                 turn_pe(2, 0, 2)
@@ -380,7 +376,7 @@ def tile_head_kernel(tc, f0, f1, f2, w0, b0, w1, b1, w2, b2, anchors, out_0, out
                 turn_pe(1, 0, 2)
             if c + 2 < 5:
                 inter_s(c + 2)
-            if c == -1:
+            if c == 0:
                 spread_b_s()
             if c == 1:
                 inter_s(5)
@@ -391,9 +387,6 @@ def tile_head_kernel(tc, f0, f1, f2, w0, b0, w1, b1, w2, b2, anchors, out_0, out
                 turn_s(1, 0, 2)
                 turn_pe(1, 2, 1)
                 turn_s(1, 2, 1)
-            if c == 2:
-                casts(0)
-                store1(0)
             if c in (3, 4):
                 casts(c - 1)
                 store1(c - 1)
@@ -417,6 +410,6 @@ def tile_head_kernel(tc, f0, f1, f2, w0, b0, w1, b1, w2, b2, anchors, out_0, out
                 sig(c)
                 fixv(c)
                 store0(c)
-            if c in (2, 5):
+            if c in (1, 2, 5):
                 casts(c - 1)
                 store1(c - 1)

@@ -19,19 +19,14 @@ P = 128
 NA = 3
 NO = 128
 Y_SCALE = 190.0
-MANUAL = True
-V_SHARE = [64, 72, 48, 48]
-V_CASTS = [(4, 1), (4, 2)]
 
 
 def tile_head_kernel(tc, f0, f1, f2, w0, b0, w1, b1, w2, b2, anchors, out_0, out_1):
     nc = tc.nc
     with ExitStack() as ctx:
         keep = ctx.enter_context(tc.tile_pool(name="keep", bufs=1))
-        ps_mm = ctx.enter_context(tc.psum_pool(name="ps_mm", bufs=6))
-        ps_xt = ctx.enter_context(tc.psum_pool(name="ps_xt", bufs=2))
-        if MANUAL:
-            ctx.enter_context(tc.manual_schedule())
+        ps = ctx.enter_context(tc.psum_pool(name="ps", bufs=1))
+        ctx.enter_context(tc.manual_schedule())
 
         raw00a = keep.tile([P, 4, 256], BF16, name="raw00a")
         raw00b = keep.tile([P, 4, 256], BF16, name="raw00b")
@@ -69,45 +64,50 @@ def tile_head_kernel(tc, f0, f1, f2, w0, b0, w1, b1, w2, b2, anchors, out_0, out
         f0n1 = f0[1].rearrange("(p j) u v -> p j (u v)", j=4)
         anc = anchors.rearrange("(o l) a w -> o (l a w)", o=1)
         w0v = w0.rearrange("(a r) k -> r a k", a=NA)
-        if True:
-            nc.sync.dma_start(out=wr0[:, 0:2], in_=w0v[:, 0:2])
-            nc.sync.dma_start(out=raw00a[:], in_=f0n0[:, :, 0:256])
-            nc.sync.dma_start(out=wr0[:, 2:3], in_=w0v[:, 2:3])
-            nc.sync.dma_start(out=raw00b[:], in_=f0n0[:, :, 256:512])
-            nc.sync.dma_start(out=rows_a[0:1, 0:384], in_=b0.rearrange("(o c) -> o c", o=1))
-            nc.sync.dma_start(out=rows_a[0:1, 384:396], in_=anc[:, 0:12])
-            nc.sync.dma_start(out=raw01[:], in_=f0n0[:, :, 512:1024])
-            nc.sync.dma_start(out=raw1x[:], in_=f0n1)
-            nc.sync.dma_start(out=rows_b[0:1, 0:384], in_=b1.rearrange("(o c) -> o c", o=1))
-            nc.sync.dma_start(out=rows_b[0:1, 384:640], in_=b2[0:256].rearrange("(o c) -> o c", o=1))
-            nc.sync.dma_start(out=rows_b[64:65, 384:640], in_=b2[128:384].rearrange("(o c) -> o c", o=1))
-            nc.sync.dma_start(out=rows_b[0:1, 640:644], in_=anc[:, 12:16])
-            nc.sync.dma_start(out=rows_b[64:65, 640:644], in_=anc[:, 14:18])
-            nc.sync.dma_start(out=wr2[:], in_=w2.rearrange("(a r) k -> r a k", a=NA))
-            for n in range(2):
-                nc.sync.dma_start(
-                    out=rawl2[:, n].rearrange("p k j x -> p k (j x)"),
-                    in_=f2[n].rearrange("(k p j) u v -> p k (j u v)", k=2, j=4),
-                )
-            nc.sync.dma_start(out=wr1[:], in_=w1.rearrange("(a r) k -> r a k", a=NA))
+        nc.sync.dma_start(out=wr0[:, 0:2], in_=w0v[:, 0:2])
+        nc.sync.dma_start(out=raw00a[:], in_=f0n0[:, :, 0:256])
+        nc.sync.dma_start(out=wr0[:, 2:3], in_=w0v[:, 2:3])
+        nc.sync.dma_start(out=raw00b[:], in_=f0n0[:, :, 256:512])
+        nc.sync.dma_start(out=rows_a[0:1, 0:384], in_=b0.rearrange("(o c) -> o c", o=1))
+        nc.sync.dma_start(out=rows_a[0:1, 384:396], in_=anc[:, 0:12])
+        nc.sync.dma_start(out=raw01[:], in_=f0n0[:, :, 512:1024])
+        nc.sync.dma_start(out=raw1x[:], in_=f0n1)
+        nc.sync.dma_start(out=rows_b[0:1, 0:384], in_=b1.rearrange("(o c) -> o c", o=1))
+        nc.sync.dma_start(out=rows_b[0:1, 384:640], in_=b2[0:256].rearrange("(o c) -> o c", o=1))
+        nc.sync.dma_start(out=rows_b[64:65, 384:640], in_=b2[128:384].rearrange("(o c) -> o c", o=1))
+        nc.sync.dma_start(out=rows_b[0:1, 640:644], in_=anc[:, 12:16])
+        nc.sync.dma_start(out=rows_b[64:65, 640:644], in_=anc[:, 14:18])
+        nc.sync.dma_start(out=wr1[:], in_=w1.rearrange("(a r) k -> r a k", a=NA))
+        nc.sync.dma_start(
+            out=rawl1[:].rearrange("p n j x -> p n (j x)"),
+            in_=f1.rearrange("n (p j) u v -> p n (j u v)", j=4),
+        )
+        nc.sync.dma_start(out=wr2[:], in_=w2.rearrange("(a r) k -> r a k", a=NA))
+        for n in range(2):
             nc.sync.dma_start(
-                out=rawl1[:].rearrange("p n j x -> p n (j x)"),
-                in_=f1.rearrange("n (p j) u v -> p n (j u v)", j=4),
+                out=rawl2[:, n].rearrange("p k j x -> p k (j x)"),
+                in_=f2[n].rearrange("(k p j) u v -> p k (j u v)", k=2, j=4),
             )
 
         bias = keep.tile([P, 1024], BF16, name="bias")
-        a4x = keep.tile([P, 14, 2], F32, name="a4x")
-        a4y = keep.tile([P, 14, 2], F32, name="a4y")
+        a4 = keep.tile([P, 36, 2], F32, name="a4")
+        a45 = keep.tile([P, 4, 2], F32, name="a45")
 
         def times4(dst, src):
             nc.scalar.activation(out=dst, in_=src, func=ACT.Copy, scale=4.0)
 
         held = {}
+        xt_count = [0]
+
+        def xt_tile(shape, dtype):
+            xt_count[0] += 1
+            xt = ps.tile(shape, dtype, tag="x%d" % (xt_count[0] % 2))
+            return xt
 
         def spread_a_pe():
-            pb = ps_xt.tile([P, 384], BF16, tag="xt")
+            pb = xt_tile([P, 384], BF16)
             nc.tensor.matmul(out=pb[:], lhsT=ones[:], rhs=rows_a[:, 0:384], start=True, stop=True)
-            pa = ps_xt.tile([P, 12], F32, tag="xt")
+            pa = xt_tile([P, 12], F32)
             nc.tensor.matmul(out=pa[:], lhsT=ones[:], rhs=rows_a[:, 384:396], start=True, stop=True)
             held["pb_a"] = pb
             held["pa_a"] = pa
@@ -118,14 +118,15 @@ def tile_head_kernel(tc, f0, f1, f2, w0, b0, w1, b1, w2, b2, anchors, out_0, out
             nc.scalar.copy(out=bias[:, 0:384], in_=pb[:])
             lv0 = pa[:, 0:6].rearrange("p (a w) -> p a w", w=2).unsqueeze(2).to_broadcast([P, NA, 4, 2])
             lv1 = pa[:, 6:12].rearrange("p (a w) -> p a w", w=2).unsqueeze(2).to_broadcast([P, NA, 4, 2])
-            times4(a4x[:, 0:12, :].rearrange("p (a g) w -> p a g w", g=4), lv0)
-            times4(a4y[:, 0:12, :].rearrange("p (a g) w -> p a g w", g=4), lv1)
+            times4(a4[:, 0:12, :].rearrange("p (a g) w -> p a g w", g=4), lv0)
+            times4(a4[:, 12:24, :].rearrange("p (a g) w -> p a g w", g=4), lv0)
+            times4(a4[:, 24:36, :].rearrange("p (a g) w -> p a g w", g=4), lv1)
 
         def spread_b_pe():
-            pb = ps_xt.tile([P, 640], BF16, tag="xt")
+            pb = xt_tile([P, 640], BF16)
             nc.tensor.matmul(out=pb[:, 0:384], lhsT=ones[:], rhs=rows_b[:, 0:384], start=True, stop=True)
             nc.tensor.matmul(out=pb[:, 384:640], lhsT=halves[:], rhs=rows_b[:, 384:640], start=True, stop=True)
-            pa = ps_xt.tile([P, 4], F32, tag="xt")
+            pa = xt_tile([P, 4], F32)
             nc.tensor.matmul(out=pa[:], lhsT=halves[:], rhs=rows_b[:, 640:644], start=True, stop=True)
             held["pb_b"] = pb
             held["pa_b"] = pa
@@ -134,8 +135,8 @@ def tile_head_kernel(tc, f0, f1, f2, w0, b0, w1, b1, w2, b2, anchors, out_0, out
             pb = held["pb_b"]
             pa = held["pa_b"]
             nc.scalar.copy(out=bias[:, 384:1024], in_=pb[:])
-            times4(a4x[:, 12:14, :], pa[:, 0:2].unsqueeze(1).to_broadcast([P, 2, 2]))
-            times4(a4y[:, 12:14, :], pa[:, 2:4].unsqueeze(1).to_broadcast([P, 2, 2]))
+            times4(a45[:, 0:2, :], pa[:, 0:2].unsqueeze(1).to_broadcast([P, 2, 2]))
+            times4(a45[:, 2:4, :], pa[:, 2:4].unsqueeze(1).to_broadcast([P, 2, 2]))
 
         wraws = [wr0, wr1, wr2]
         wq = []
@@ -152,7 +153,7 @@ def tile_head_kernel(tc, f0, f1, f2, w0, b0, w1, b1, w2, b2, anchors, out_0, out
 
         def turn_pe(lv, q0, nq):
             words = wraws[lv][:].bitcast(F32)
-            xt = ps_xt.tile([P, 2, 2, NO], F32, tag="xt")
+            xt = xt_tile([P, 2, 2, NO], F32)
             for i in range(nq):
                 kp, a = divmod(q0 + i, NA)
                 for u in range(2):
@@ -176,78 +177,105 @@ def tile_head_kernel(tc, f0, f1, f2, w0, b0, w1, b1, w2, b2, anchors, out_0, out
                 in_=flat[:, q0 * 4 * NO : (q0 + nq) * 4 * NO],
             )
 
-        fg = []
+        fg0 = keep.tile([P, 4, P, 4], BF16, name="fg0", align_bytes=64)
+        fg1 = keep.tile([P, 4, P, 4], BF16, name="fg1", align_bytes=64)
+        fgb = {}
         fq = []
         fs = []
         for c in range(5):
-            fg_t = keep.tile([P, 4, P, 4], BF16, name="fg_%d" % c, align_bytes=64)
+            if c > 1:
+                fgb_t = keep.tile([P, 2, P, 4], BF16, name="fgb_%d" % c, align_bytes=64)
+                fgb[c] = fgb_t
             fq_t = keep.tile([P, 512], U32, name="fq_%d" % c, align_bytes=64)
             fs_t = keep.tile([P, 512], U8, name="fs_%d" % c, align_bytes=64)
-            fg.append(fg_t)
             fq.append(fq_t)
             fs.append(fs_t)
-        fg.append(fg2)
-        fq.append(fq2)
-        fs.append(fs2)
-        n_rows = [12, 12, 12, 14, 14]
-        og = []
-        qg = []
-        for g in range(5):
-            o_t = keep.tile([P, n_rows[g], NO], F32, name="o_%d" % g)
-            q_t = keep.tile([P, n_rows[g] * NO], FP8, name="q_%d" % g)
-            og.append(o_t)
-            qg.append(q_t)
+        og = keep.tile([P, 60, NO], F32, name="og")
+        qg = keep.tile([P, 60 * NO], FP8, name="qg")
+        og5 = keep.tile([P, 4, NO], F32, name="og5")
+        qg5 = keep.tile([P, 4 * NO], FP8, name="qg5")
 
         def walk(dst, src, g):
             return (dst.rearrange("p g m j -> p m g j"), src.rearrange("p j (m g) -> p m g j", g=g))
 
-        def pieces(c):
-            if c == 0:
-                return [
-                    walk(fg[0][:, :, 0:64, :], raw00a[:], 4),
-                    walk(fg[0][:, :, 64:128, :], raw00b[:], 4),
-                ]
-            if c < 4:
-                src = [raw01[:], raw1x[:, :, 0:512], raw1x[:, :, 512:1024]][c - 1]
-                mv = V_SHARE[c]
-                mid = (mv + P) // 2
-                return [
-                    walk(fg[c][:, :, 0:mv, :], src[:, :, 0 : 4 * mv], 4),
-                    walk(fg[c][:, :, mv:mid, :], src[:, :, 4 * mv : 4 * mid], 4),
-                    walk(fg[c][:, :, mid:P, :], src[:, :, 4 * mid : 4 * P], 4),
-                ]
-            if c == 4:
-                return [
-                    walk(fg[4][:, 0:2], rawl1[:, 0], 2),
-                    walk(fg[4][:, 2:4, 0:64, :], rawl1[:, 1, :, 0:128], 2),
-                    walk(fg[4][:, 2:4, 64:128, :], rawl1[:, 1, :, 128:256], 2),
-                ]
+        def half(c, h):
+            dst = (fg1[:, 0:2] if h == 0 else fgb[c][:]).rearrange("p g m j -> p m g j")
+            if c != 3:
+                src = raw1x[:, :, 0:512] if c == 2 else raw1x[:, :, 512:1024]
+                return (dst, src.rearrange("p j (m g) -> p m g j", g=4)[:, :, 2 * h : 2 * h + 2, :])
+            return (dst, rawl1[:, h].rearrange("p j (m g) -> p m g j", g=2))
+
+        def inter0_v():
+            o_ap, i_ap = walk(fg0[:, :, 0:64, :], raw00a[:], 4)
+            nc.vector.tensor_copy(out=o_ap, in_=i_ap)
+
+        def inter0_b(on_vector):
+            o_ap, i_ap = walk(fg0[:, :, 64:128, :], raw00b[:], 4)
+            if on_vector:
+                nc.vector.tensor_copy(out=o_ap, in_=i_ap)
+            else:
+                nc.scalar.copy(out=o_ap, in_=i_ap)
+
+        def inter1(h, on_vector):
+            o_ap = fg1[:, 2 * h : 2 * h + 2].rearrange("p g m j -> p m g j")
+            i_ap = raw01[:].rearrange("p j (m g) -> p m g j", g=4)[:, :, 2 * h : 2 * h + 2, :]
+            if on_vector:
+                nc.vector.tensor_copy(out=o_ap, in_=i_ap)
+            else:
+                nc.scalar.copy(out=o_ap, in_=i_ap)
+
+        def inter_g(c):
+            o_ap, i_ap = half(c, 0)
+            nc.gpsimd.tensor_scalar(out=o_ap, in0=i_ap, scalar1=1.0, scalar2=0.0, op0=ALU.mult, op1=ALU.add)
+
+        def inter_s(c):
+            o_ap, i_ap = half(c, 1)
+            nc.scalar.copy(out=o_ap, in_=i_ap)
+
+        def l2_pieces():
             dst = fg2[:].rearrange("p (q z) x j -> p q z x j", z=2)[:, :, 1]
             sv = rawl2[:].rearrange("p n k j x -> p (n k) x j")
             return [(dst[:, 0:1], sv[:, 0:1]), (dst[:, 1:4], sv[:, 1:4])]
 
-        def inter_v(c):
-            pc = pieces(c)
-            nc.vector.tensor_copy(out=pc[0][0], in_=pc[0][1])
+        def inter5_v():
+            o_ap, i_ap = l2_pieces()[0]
+            nc.vector.tensor_copy(out=o_ap, in_=i_ap)
 
-        def inter_s(c):
-            for o_ap, i_ap in pieces(c)[1:]:
-                nc.scalar.copy(out=o_ap, in_=i_ap)
+        def inter5_s():
+            o_ap, i_ap = l2_pieces()[1]
+            nc.scalar.copy(out=o_ap, in_=i_ap)
 
         def quant(c):
-            if c < 5:
-                flat = fg[c][:].rearrange("p g m j -> p (g m j)")
-            else:
-                flat = fg2[:].rearrange("p b x j -> p (b x j)")
-            nc.vector.quantize_mx(out=fq[c][:, 0:512].bitcast(FP8X4), scales=fs[c][:, 0:512], in_=flat)
+            if c < 2:
+                nc.vector.quantize_mx(
+                    out=fq[c][:].bitcast(FP8X4), scales=fs[c][:], in_=[fg0, fg1][c][:].rearrange("p g m j -> p (g m j)")
+                )
+            elif c == 5:
+                nc.vector.quantize_mx(
+                    out=fq2[:, 0:512].bitcast(FP8X4), scales=fs2[:, 0:512], in_=fg2[:].rearrange("p b x j -> p (b x j)")
+                )
+
+        def quant_b(c):
+            nc.vector.quantize_mx(
+                out=fq[c][:, 256:512].bitcast(FP8X4),
+                scales=fs[c][:, 256:512],
+                in_=fgb[c][:].rearrange("p g m j -> p (g m j)"),
+            )
+
+        def quant_a(c):
+            nc.vector.quantize_mx(
+                out=fq[c][:, 0:256].bitcast(FP8X4),
+                scales=fs[c][:, 0:256],
+                in_=fg1[:, 0:2].rearrange("p g m j -> p (g m j)"),
+            )
 
         banks = {}
 
         def mm(c):
             if c < 5:
-                lv = 0 if c < 4 else 1
+                lv = 1 if c == 3 else 0
                 for a in range(NA):
-                    acc = ps_mm.tile([P, 4, NO], F32, tag="acc")
+                    acc = ps.tile([P, 4, NO], F32, tag="%s%d" % ("eo"[c % 2], a))
                     for s in range(4):
                         nc.tensor.matmul_mx(
                             out=acc[:, s, :],
@@ -260,17 +288,17 @@ def tile_head_kernel(tc, f0, f1, f2, w0, b0, w1, b1, w2, b2, anchors, out_0, out
                         )
                     banks[(c, a)] = acc
             else:
+                acc = xt_tile([P, 2, 2, NO], F32)
                 for t in range(2):
-                    acc = ps_mm.tile([P, 2, NO], F32, tag="acc")
                     for n in range(2):
                         todo = []
-                        for half in range(2):
+                        for hf in range(2):
                             for kp in range(2):
-                                todo.append(((2 * (2 * n + kp) + 1 - half) * 64, (kp * NA + t + half) * NO))
+                                todo.append(((2 * (2 * n + kp) + 1 - hf) * 64, (kp * NA + t + hf) * NO))
                         for i in range(4):
                             fc, wc = todo[i]
                             nc.tensor.matmul_mx(
-                                out=acc[:, n, :],
+                                out=acc[:, t, n, :],
                                 lhsT=fq2[:, fc : fc + P].bitcast(FP8X4),
                                 lhsT_scale=fs2[:, fc : fc + P],
                                 rhs=wq[2][:, wc : wc + NO].bitcast(FP8X4),
@@ -278,138 +306,210 @@ def tile_head_kernel(tc, f0, f1, f2, w0, b0, w1, b1, w2, b2, anchors, out_0, out
                                 start=(i == 0),
                                 stop=(i == 3),
                             )
-                    banks[(c, t)] = acc
+                banks[5] = acc
 
-        def add_bias(dst, acc, col, reps):
+        def badd(c, a):
+            col = (384 if c == 3 else 0) + a * NO
             nc.vector.tensor_tensor(
-                out=dst,
-                in0=acc[:],
-                in1=bias[:, col : col + NO].unsqueeze(1).to_broadcast([P, reps, NO]),
+                out=og[:, 12 * c + 4 * a : 12 * c + 4 * a + 4, :],
+                in0=banks[(c, a)][:],
+                in1=bias[:, col : col + NO].unsqueeze(1).to_broadcast([P, 4, NO]),
                 op=ALU.add,
             )
 
-        def badd(c):
-            for a in range(NA):
-                add_bias(og[c][:, 4 * a : 4 * a + 4, :], banks[(c, a)], (0 if c < 4 else 384) + a * NO, 4)
-            if c >= 3:
-                add_bias(og[c][:, 12:14, :], banks[(5, c - 3)], 768 + NO * (c - 3), 2)
+        def badd5():
+            nc.vector.tensor_tensor(
+                out=og5[:].rearrange("p (t n) j -> p t n j", t=2),
+                in0=banks[5][:],
+                in1=bias[:, 768:1024].rearrange("p (t j) -> p t j", t=2).unsqueeze(2).to_broadcast([P, 2, 2, NO]),
+                op=ALU.add,
+            )
 
         sgs = {}
 
-        def sig(g):
-            sg = keep.tile([P, n_rows[g], 4], F32, name="sg%d" % g)
-            nc.scalar.activation(out=sg[:], in_=og[g][:, :, 0:4], func=ACT.Sigmoid)
-            sgs[g] = sg
+        def sig(r0, r1):
+            n = r1 - r0 if r0 >= 0 else 4
+            sg = keep.tile([P, n, 4], F32, name="sg%d" % (r0 + 1))
+            src = og[:, r0:r1, 0:4] if r0 >= 0 else og5[:, :, 0:4]
+            nc.scalar.activation(out=sg[:], in_=src, func=ACT.Sigmoid)
+            sgs[r0] = sg
 
-        def fixv(g):
-            sg = sgs[g]
-            rv = og[g]
-            av = a4y[:] if g == 4 else a4x[:, 0 : n_rows[g], :]
-            sa = keep.tile([P, n_rows[g], 2], F32, name="sa%d" % g)
+        def fixv(r0, r1):
+            sg = sgs[r0]
+            if r0 >= 0:
+                rv = og[:, r0:r1]
+                z = r0 % 12 + (24 if r0 // 12 == 3 else 0)
+                av = a4[:, z : z + r1 - r0, :]
+            else:
+                rv = og5[:]
+                av = a45[:]
+            n = r1 - r0 if r0 >= 0 else 4
+            sa = keep.tile([P, n, 2], F32, name="sa%d" % (r0 + 1))
             nc.vector.tensor_tensor(out=sa[:], in0=sg[:, :, 2:4], in1=av, op=ALU.mult)
             nc.vector.tensor_scalar(
                 out=rv[:, :, 0:2], in0=sg[:, :, 0:2], scalar1=2.0, scalar2=-0.5, op0=ALU.mult, op1=ALU.add
             )
             nc.vector.tensor_tensor(out=rv[:, :, 2:4], in0=sa[:], in1=sg[:, :, 2:4], op=ALU.mult)
 
-        cuts = [[0, 4, 8, 12], [0, 4, 8, 12], [0, 4, 8, 12], [0, 4, 8, 14], [0, 4, 8, 14]]
-
-        def cast(g, piece):
-            c0 = cuts[g][piece] * NO
-            c1 = cuts[g][piece + 1] * NO
-            src = og[g][:].rearrange("p r j -> p (r j)")[:, c0:c1]
-            dst = qg[g][:, c0:c1]
-            if (g, piece) in V_CASTS:
+        def cast(r0, r1, on_vector):
+            if r0 >= 0:
+                src = og[:].rearrange("p r j -> p (r j)")[:, r0 * NO : r1 * NO]
+                dst = qg[:, r0 * NO : r1 * NO]
+            else:
+                src = og5[:].rearrange("p r j -> p (r j)")
+                dst = qg5[:]
+            if on_vector:
                 nc.vector.tensor_scalar(
                     out=dst, in0=src, scalar1=Y_SCALE, scalar2=None, op0=ALU.mult, saturate=False
                 )
             else:
                 nc.scalar.activation(out=dst, in_=src, func=ACT.Copy, scale=Y_SCALE, saturate=False)
 
-        def stores(g, out, flat):
-            if g < 4:
-                n, h = divmod(g, 2)
+        def stores(c, out, flat, a0, a1):
+            na = a1 - a0
+            part = flat[:, (12 * c + 4 * a0) * NO : (12 * c + 4 * a1) * NO]
+            if c != 3:
+                n, h = divmod(min(c, 3), 2)
                 v = out[n, 0:3072, :].rearrange("(a h m g) j -> h m a (g j)", a=NA, h=2, m=P, g=4)
-                nc.sync.dma_start(out=v[h], in_=flat[:, 0 : 12 * NO].rearrange("p (a x) -> p a x", a=NA))
+                nc.sync.dma_start(out=v[h][:, a0:a1], in_=part.rearrange("p (a x) -> p a x", a=na))
             else:
-                s = flat[:, 0 : 12 * NO].rearrange("p (a n x) -> p n a x", a=NA, n=2)
+                s = part.rearrange("p (a n x) -> p n a x", a=na, n=2)
                 for n in range(2):
                     nc.sync.dma_start(
-                        out=out[n, 3072:3840, :].rearrange("(a m g) j -> m a (g j)", a=NA, m=P, g=2),
+                        out=out[n, 3072:3840, :].rearrange("(a m g) j -> m a (g j)", a=NA, m=P, g=2)[:, a0:a1],
                         in_=s[:, n],
                     )
-            if g >= 3:
-                r0 = 3840 + 64 * (g - 3)
-                nc.sync.dma_start(
-                    out=out[:, r0 : r0 + P, :].rearrange("n m j -> m n j"),
-                    in_=flat[:, 12 * NO : 14 * NO].rearrange("p (n j) -> p n j", n=2),
-                )
 
-        def store0(g):
-            stores(g, out_0, og[g][:].rearrange("p r j -> p (r j)"))
+        def stores5(t, out, flat):
+            r0 = 3840 + 64 * t
+            nc.sync.dma_start(
+                out=out[:, r0 : r0 + P, :].rearrange("n m j -> m n j"),
+                in_=flat[:, 2 * t * NO : (2 * t + 2) * NO].rearrange("p (n j) -> p n j", n=2),
+            )
 
-        def store1(g):
-            stores(g, out_1, qg[g][:].bitcast(U8))
+        def store0(c, a0=0, a1=NA):
+            stores(c, out_0, og[:].rearrange("p r j -> p (r j)"), a0, a1)
 
-        def casts(g):
-            for piece in range(len(cuts[g]) - 1):
-                cast(g, piece)
+        def store1(c, a0=0, a1=NA):
+            stores(c, out_1, qg[:].bitcast(U8), a0, a1)
+
+        def store0_5(t):
+            if t == 0:
+                stores5(0, out_0, og5[:].rearrange("p r j -> p (r j)"))
+            else:
+                nc.sync.dma_start(out=out_0[:, 3968:4032, :].rearrange("n m j -> m n j"), in_=og5[64:128, 2:4, :])
+
+        def store1_5(t):
+            stores5(t, out_1, qg5[:].bitcast(U8))
 
         turn_pe(0, 0, 2)
         turn_pe(0, 2, 1)
         turn_s(0, 0, 2)
-        inter_v(0)
-        inter_s(0)
         turn_s(0, 2, 1)
+        inter0_v()
         weights_quant(0, 0, 2)
+        inter0_b(True)
         weights_quant(0, 2, 1)
         spread_a_pe()
         spread_a_s()
-        for c in range(-1, 6):
-            if c == 0:
-                spread_b_pe()
-            if c == 1:
-                turn_pe(2, 0, 2)
-                turn_pe(2, 2, 2)
-            if c == 2:
-                turn_pe(2, 4, 2)
-                turn_pe(1, 0, 2)
-            if c + 2 < 5:
-                inter_s(c + 2)
-            if c == 0:
-                spread_b_s()
-            if c == 1:
-                inter_s(5)
-                turn_s(2, 0, 2)
-                turn_s(2, 2, 2)
-            if c == 2:
-                turn_s(2, 4, 2)
-                turn_s(1, 0, 2)
-                turn_pe(1, 2, 1)
-                turn_s(1, 2, 1)
-            if c in (3, 4):
-                casts(c - 1)
-                store1(c - 1)
-            if 0 <= c < 5:
-                badd(c)
-            if c + 1 < 5:
-                quant(c + 1)
-                mm(c + 1)
-            if c == 1:
-                inter_v(5)
-            if c == 2:
-                weights_quant(2, 0, 4)
-                weights_quant(2, 4, 2)
-                quant(5)
-                mm(5)
-                weights_quant(1, 0, 2)
-                weights_quant(1, 2, 1)
-            if c + 2 < 5:
-                inter_v(c + 2)
-            if 0 <= c < 5:
-                sig(c)
-                fixv(c)
-                store0(c)
-            if c in (1, 2, 5):
-                casts(c - 1)
-                store1(c - 1)
+        quant(0)
+        mm(0)
+        spread_b_pe()
+        inter1(1, False)
+        inter1(0, True)
+        quant(1)
+        mm(1)
+        inter_s(2)
+        inter_g(2)
+        spread_b_s()
+        turn_pe(1, 0, 2)
+        turn_pe(1, 2, 1)
+        badd(0, 0)
+        badd(0, 1)
+        badd(0, 2)
+        sig(0, 12)
+        quant_b(2)
+        inter_s(3)
+        fixv(0, 12)
+        store0(0)
+        quant_a(2)
+        mm(2)
+        inter_g(3)
+        turn_s(1, 0, 2)
+        turn_pe(2, 0, 2)
+        turn_s(1, 2, 1)
+        turn_pe(2, 2, 2)
+        cast(0, 4, False)
+        badd(1, 0)
+        badd(1, 1)
+        badd(1, 2)
+        sig(12, 24)
+        quant_b(3)
+        turn_s(2, 0, 2)
+        turn_pe(2, 4, 2)
+        inter_s(4)
+        weights_quant(1, 0, 2)
+        weights_quant(1, 2, 1)
+        fixv(12, 24)
+        store0(1)
+        quant_a(3)
+        mm(3)
+        inter_g(4)
+        turn_s(2, 2, 2)
+        cast(4, 8, False)
+        badd(2, 0)
+        badd(2, 1)
+        badd(2, 2)
+        sig(24, 36)
+        turn_s(2, 4, 2)
+        inter5_s()
+        quant_b(4)
+        fixv(24, 36)
+        store0(2)
+        weights_quant(2, 0, 4)
+        weights_quant(2, 4, 2)
+        inter5_v()
+        quant(5)
+        mm(5)
+        cast(8, 12, False)
+        store1(0)
+        cast(12, 24, False)
+        store1(1)
+        badd(3, 0)
+        badd(3, 1)
+        badd(3, 2)
+        sig(36, 48)
+        quant_a(4)
+        mm(4)
+        fixv(36, 48)
+        store0(3)
+        cast(24, 36, False)
+        store1(2)
+        badd5()
+        sig(-1, 0)
+        cast(36, 40, True)
+        fixv(-1, 0)
+        store0_5(0)
+        store0_5(1)
+        cast(-1, 0, False)
+        store1_5(0)
+        badd(4, 0)
+        sig(48, 52)
+        badd(4, 1)
+        cast(40, 44, False)
+        sig(52, 56)
+        fixv(48, 52)
+        store0(4, 0, 1)
+        badd(4, 2)
+        cast(44, 48, False)
+        store1(3)
+        sig(56, 60)
+        fixv(52, 56)
+        store0(4, 1, 2)
+        cast(48, 52, True)
+        fixv(56, 60)
+        store0(4, 2, 3)
+        cast(52, 56, False)
+        cast(56, 60, True)
+        store1(4)
+        store1_5(1)

@@ -42,7 +42,6 @@ def tile_head_kernel(tc, f0, f1, f2, w0, b0, w1, b1, w2, b2, anchors, out_0, out
         ones = keep.tile([P, P], BF16, name="ones")
         halves = keep.tile([P, P], BF16, name="halves")
         ident = keep.tile([P, P], F32, name="ident")
-        fg2 = keep.tile([P, 8, 64, 4], BF16, name="fg2", align_bytes=64)
         fq2 = keep.tile([P, 576], U32, name="fq2", align_bytes=64)
         fs2 = keep.tile([P, 576], U8, name="fs2", align_bytes=64)
         warm = keep.tile([P, 2], F32, name="warm")
@@ -54,10 +53,9 @@ def tile_head_kernel(tc, f0, f1, f2, w0, b0, w1, b1, w2, b2, anchors, out_0, out
         nc.gpsimd.memset(halves[:], 0.0)
         nc.gpsimd.memset(halves[0:64, 0:64], 1.0)
         nc.gpsimd.memset(halves[64:128, 64:128], 1.0)
-        nc.gpsimd.memset(fg2[:].rearrange("p b x j -> p (b x j)").bitcast(F32), 0.0)
         nc.vector.memset(warm[:], 0.0)
-        nc.vector.memset(fq2[:, 512:576].bitcast(I32), 0)
-        nc.vector.memset(fs2[:, 512:576].bitcast(I32), 0)
+        nc.vector.memset(fq2[:].bitcast(I32), 0)
+        nc.vector.memset(fs2[:].bitcast(I32), 0)
         nc.scalar.activation(out=warm[:, 1:2], in_=warm[:, 0:1], func=ACT.Sigmoid)
 
         f0n0 = f0[0].rearrange("(p j) u v -> p j (u v)", j=4)
@@ -232,27 +230,31 @@ def tile_head_kernel(tc, f0, f1, f2, w0, b0, w1, b1, w2, b2, anchors, out_0, out
             o_ap, i_ap = half(c, 1)
             nc.scalar.copy(out=o_ap, in_=i_ap)
 
-        def l2_pieces():
-            dst = fg2[:].rearrange("p (q z) x j -> p q z x j", z=2)[:, :, 1]
-            sv = rawl2[:].rearrange("p n k j x -> p (n k) x j")
-            return [(dst[:, 0:1], sv[:, 0:1]), (dst[:, 1:4], sv[:, 1:4])]
+        def inter5_g():
+            dst = fg1[:, 0:2].rearrange("p g m j -> p (g m j)").rearrange("p (q x j) -> p q x j", q=4, j=4)
+            nc.gpsimd.tensor_scalar(
+                out=dst,
+                in0=rawl2[:].rearrange("p n k j x -> p (n k) x j"),
+                scalar1=1.0,
+                scalar2=0.0,
+                op0=ALU.mult,
+                op1=ALU.add,
+            )
 
-        def inter5_v():
-            o_ap, i_ap = l2_pieces()[0]
-            nc.vector.tensor_copy(out=o_ap, in_=i_ap)
-
-        def inter5_s():
-            o_ap, i_ap = l2_pieces()[1]
-            nc.scalar.copy(out=o_ap, in_=i_ap)
+        def quant5():
+            flat = fg1[:, 0:2].rearrange("p g m j -> p (g m j)")
+            for q in range(4):
+                c0 = (2 * q + 1) * 64
+                nc.vector.quantize_mx(
+                    out=fq2[:, c0 : c0 + 64].bitcast(FP8X4),
+                    scales=fs2[:, c0 : c0 + 64],
+                    in_=flat[:, 256 * q : 256 * (q + 1)],
+                )
 
         def quant(c):
             if c < 2:
                 nc.vector.quantize_mx(
                     out=fq[c][:].bitcast(FP8X4), scales=fs[c][:], in_=[fg0, fg1][c][:].rearrange("p g m j -> p (g m j)")
-                )
-            elif c == 5:
-                nc.vector.quantize_mx(
-                    out=fq2[:, 0:512].bitcast(FP8X4), scales=fs2[:, 0:512], in_=fg2[:].rearrange("p b x j -> p (b x j)")
                 )
 
         def quant_b(c):
@@ -447,42 +449,40 @@ def tile_head_kernel(tc, f0, f1, f2, w0, b0, w1, b1, w2, b2, anchors, out_0, out
         quant_b(3)
         turn_s(2, 0, 2)
         turn_pe(2, 4, 2)
-        inter_s(4)
         weights_quant(1, 0, 2)
         weights_quant(1, 2, 1)
         fixv(12, 24)
         store0(1)
         quant_a(3)
         mm(3)
-        inter_g(4)
+        inter5_g()
         turn_s(2, 2, 2)
-        cast(4, 8, False)
+        cast(4, 12, False)
+        store1(0)
+        turn_s(2, 4, 2)
         badd(2, 0)
         badd(2, 1)
         badd(2, 2)
         sig(24, 36)
-        turn_s(2, 4, 2)
-        inter5_s()
-        quant_b(4)
+        weights_quant(2, 0, 4)
         fixv(24, 36)
         store0(2)
-        weights_quant(2, 0, 4)
         weights_quant(2, 4, 2)
-        inter5_v()
-        quant(5)
+        quant5()
         mm(5)
-        cast(8, 12, False)
-        store1(0)
+        inter_g(4)
+        inter_s(4)
         cast(12, 24, False)
         store1(1)
         badd(3, 0)
         badd(3, 1)
         badd(3, 2)
         sig(36, 48)
-        quant_a(4)
-        mm(4)
+        quant_b(4)
         fixv(36, 48)
         store0(3)
+        quant_a(4)
+        mm(4)
         cast(24, 36, False)
         store1(2)
         badd5()

@@ -67,7 +67,7 @@ def tile_head_kernel(tc, f0, f1, f2, w0, b0, w1, b1, w2, b2, anchors, out_0, out
         nc.sync.dma_start(out=wr0[:, 2:3], in_=w0v[:, 2:3])
         nc.sync.dma_start(out=raw00b[:], in_=f0n0[:, :, 256:512])
         nc.sync.dma_start(out=rows_a[0:1, 0:384], in_=b0.rearrange("(o c) -> o c", o=1))
-        nc.sync.dma_start(out=rows_a[0:1, 384:396], in_=anc[:, 0:12])
+        nc.sync.dma_start(out=rows_a[0:1, 384:400], in_=anc[:, 0:16])
         nc.sync.dma_start(out=raw01[:], in_=f0n0[:, :, 512:1024])
         nc.sync.dma_start(out=raw1x[:], in_=f0n1)
         nc.sync.dma_start(out=rows_b[0:1, 0:384], in_=b1.rearrange("(o c) -> o c", o=1))

@@ -28,8 +28,7 @@ def tile_head_kernel(tc, f0, f1, f2, w0, b0, w1, b1, w2, b2, anchors, out_0, out
         ps = ctx.enter_context(tc.psum_pool(name="ps", bufs=1))
         ctx.enter_context(tc.manual_schedule())
 
-        raw00a = keep.tile([P, 4, 256], BF16, name="raw00a")
-        raw00b = keep.tile([P, 4, 256], BF16, name="raw00b")
+        raw00 = keep.tile([P, 4, 512], BF16, name="raw00")
         raw01 = keep.tile([P, 4, 512], BF16, name="raw01")
         raw1x = keep.tile([P, 4, 1024], BF16, name="raw1x")
         wr0 = keep.tile([P, NA, 512], BF16, name="wr0")
@@ -63,9 +62,8 @@ def tile_head_kernel(tc, f0, f1, f2, w0, b0, w1, b1, w2, b2, anchors, out_0, out
         anc = anchors.rearrange("(o l) a w -> o (l a w)", o=1)
         w0v = w0.rearrange("(a r) k -> r a k", a=NA)
         nc.sync.dma_start(out=wr0[:, 0:2], in_=w0v[:, 0:2])
-        nc.sync.dma_start(out=raw00a[:], in_=f0n0[:, :, 0:256])
+        nc.sync.dma_start(out=raw00[:], in_=f0n0[:, :, 0:512])
         nc.sync.dma_start(out=wr0[:, 2:3], in_=w0v[:, 2:3])
-        nc.sync.dma_start(out=raw00b[:], in_=f0n0[:, :, 256:512])
         nc.sync.dma_start(out=rows_a[0:1, 0:384], in_=b0.rearrange("(o c) -> o c", o=1))
         nc.sync.dma_start(out=rows_a[0:1, 384:400], in_=anc[:, 0:16])
         nc.sync.dma_start(out=raw01[:], in_=f0n0[:, :, 512:1024])
@@ -204,11 +202,11 @@ def tile_head_kernel(tc, f0, f1, f2, w0, b0, w1, b1, w2, b2, anchors, out_0, out
             return (dst, rawl1[:, h].rearrange("p j (m g) -> p m g j", g=2))
 
         def inter0_v():
-            o_ap, i_ap = walk(fg0[:, :, 0:64, :], raw00a[:], 4)
+            o_ap, i_ap = walk(fg0[:, :, 0:64, :], raw00[:, :, 0:256], 4)
             nc.vector.tensor_copy(out=o_ap, in_=i_ap)
 
         def inter0_b(on_vector):
-            o_ap, i_ap = walk(fg0[:, :, 64:128, :], raw00b[:], 4)
+            o_ap, i_ap = walk(fg0[:, :, 64:128, :], raw00[:, :, 256:512], 4)
             if on_vector:
                 nc.vector.tensor_copy(out=o_ap, in_=i_ap)
             else:

@@ -192,14 +192,14 @@ def tile_head_kernel(tc, f0, f1, f2, w0, b0, w1, b1, w2, b2, anchors, out_0, out
         qg5 = keep.tile([P, 4 * NO], FP8, name="qg5")
 
         def walk(dst, src, g):
-            return (dst.rearrange("p g m j -> p m g j"), src.rearrange("p j (m g) -> p m g j", g=g))
+            return (dst.rearrange("p g m j -> p m j g"), src.rearrange("p j (m g) -> p m j g", g=g))
 
         def half(c, h):
-            dst = (fg1[:, 0:2] if h == 0 else fgb[c][:]).rearrange("p g m j -> p m g j")
+            dst = (fg1[:, 0:2] if h == 0 else fgb[c][:]).rearrange("p g m j -> p m j g")
             if c != 3:
                 src = raw1x[:, :, 0:512] if c == 2 else raw1x[:, :, 512:1024]
-                return (dst, src.rearrange("p j (m g) -> p m g j", g=4)[:, :, 2 * h : 2 * h + 2, :])
-            return (dst, rawl1[:, h].rearrange("p j (m g) -> p m g j", g=2))
+                return (dst, src.rearrange("p j (m g) -> p m j g", g=4)[:, :, :, 2 * h : 2 * h + 2])
+            return (dst, rawl1[:, h].rearrange("p j (m g) -> p m j g", g=2))
 
         def inter0_v():
             o_ap, i_ap = walk(fg0[:, :, 0:64, :], raw00[:, :, 0:256], 4)
@@ -213,8 +213,8 @@ def tile_head_kernel(tc, f0, f1, f2, w0, b0, w1, b1, w2, b2, anchors, out_0, out
                 nc.scalar.copy(out=o_ap, in_=i_ap)
 
         def inter1(h, on_vector):
-            o_ap = fg1[:, 2 * h : 2 * h + 2].rearrange("p g m j -> p m g j")
-            i_ap = raw01[:].rearrange("p j (m g) -> p m g j", g=4)[:, :, 2 * h : 2 * h + 2, :]
+            o_ap = fg1[:, 2 * h : 2 * h + 2].rearrange("p g m j -> p m j g")
+            i_ap = raw01[:].rearrange("p j (m g) -> p m j g", g=4)[:, :, :, 2 * h : 2 * h + 2]
             if on_vector:
                 nc.vector.tensor_copy(out=o_ap, in_=i_ap)
             else:

@@ -477,15 +477,17 @@ def tile_head_kernel(tc, f0, f1, f2, w0, b0, w1, b1, w2, b2, anchors, out_0, out
         badd(3, 2)
         sig(36, 48)
         quant_b(4)
+        cast(32, 36, True)
         fixv(36, 48)
         store0(3)
         quant_a(4)
         mm(4)
-        cast(24, 36, False)
+        cast(24, 32, False)
         store1(2)
         badd5()
         sig(-1, 0)
-        cast(36, 40, True)
+        cast(36, 48, True)
+        store1(3)
         fixv(-1, 0)
         store0_5(0)
         store0_5(1)
@@ -494,13 +496,10 @@ def tile_head_kernel(tc, f0, f1, f2, w0, b0, w1, b1, w2, b2, anchors, out_0, out
         badd(4, 0)
         sig(48, 52)
         badd(4, 1)
-        cast(40, 44, False)
         sig(52, 56)
         fixv(48, 52)
         store0(4, 0, 1)
         badd(4, 2)
-        cast(44, 48, False)
-        store1(3)
         sig(56, 60)
         fixv(52, 56)
         store0(4, 1, 2)

@@ -86,7 +86,7 @@ def tile_head_kernel(tc, f0, f1, f2, w0, b0, w1, b1, w2, b2, anchors, out_0, out
             )
 
         bias = keep.tile([P, 1024], BF16, name="bias")
-        a4 = keep.tile([P, 36, 2], F32, name="a4")
+        a4 = keep.tile([P, 24, 2], F32, name="a4")
         a45 = keep.tile([P, 4, 2], F32, name="a45")
 
         def times4(dst, src):
@@ -115,8 +115,7 @@ def tile_head_kernel(tc, f0, f1, f2, w0, b0, w1, b1, w2, b2, anchors, out_0, out
             lv0 = pa[:, 0:6].rearrange("p (a w) -> p a w", w=2).unsqueeze(2).to_broadcast([P, NA, 4, 2])
             lv1 = pa[:, 6:12].rearrange("p (a w) -> p a w", w=2).unsqueeze(2).to_broadcast([P, NA, 4, 2])
             times4(a4[:, 0:12, :].rearrange("p (a g) w -> p a g w", g=4), lv0)
-            times4(a4[:, 12:24, :].rearrange("p (a g) w -> p a g w", g=4), lv0)
-            times4(a4[:, 24:36, :].rearrange("p (a g) w -> p a g w", g=4), lv1)
+            times4(a4[:, 12:24, :].rearrange("p (a g) w -> p a g w", g=4), lv1)
 
         def spread_b_pe():
             pb = xt_tile([P, 640], BF16)
@@ -334,11 +333,13 @@ def tile_head_kernel(tc, f0, f1, f2, w0, b0, w1, b1, w2, b2, anchors, out_0, out
             nc.scalar.activation(out=sg[:], in_=src, func=ACT.Sigmoid)
             sgs[r0] = sg
 
-        def fixv(r0, r1):
+        sas = {}
+
+        def fix1(r0, r1):
             sg = sgs[r0]
             if r0 >= 0:
                 rv = og[:, r0:r1]
-                z = r0 % 12 + (24 if r0 // 12 == 3 else 0)
+                z = r0 % 12 + (12 if r0 // 12 == 3 else 0)
                 av = a4[:, z : z + r1 - r0, :]
             else:
                 rv = og5[:]
@@ -349,7 +350,11 @@ def tile_head_kernel(tc, f0, f1, f2, w0, b0, w1, b1, w2, b2, anchors, out_0, out
             nc.vector.tensor_scalar(
                 out=rv[:, :, 0:2], in0=sg[:, :, 0:2], scalar1=2.0, scalar2=-0.5, op0=ALU.mult, op1=ALU.add
             )
-            nc.vector.tensor_tensor(out=rv[:, :, 2:4], in0=sa[:], in1=sg[:, :, 2:4], op=ALU.mult)
+            sas[r0] = sa
+
+        def fix2(r0, r1):
+            rv = og[:, r0:r1] if r0 >= 0 else og5[:]
+            nc.vector.tensor_tensor(out=rv[:, :, 2:4], in0=sas[r0][:], in1=sgs[r0][:, :, 2:4], op=ALU.mult)
 
         def cast(r0, r1, on_vector):
             if r0 >= 0:
@@ -430,10 +435,11 @@ def tile_head_kernel(tc, f0, f1, f2, w0, b0, w1, b1, w2, b2, anchors, out_0, out
         sig(0, 12)
         quant_b(2)
         inter_s(3)
-        fixv(0, 12)
-        store0(0)
+        fix1(0, 12)
         quant_a(2)
         mm(2)
+        fix2(0, 12)
+        store0(0)
         inter_g(3)
         turn_s(1, 0, 2)
         turn_pe(2, 0, 2)
@@ -448,8 +454,9 @@ def tile_head_kernel(tc, f0, f1, f2, w0, b0, w1, b1, w2, b2, anchors, out_0, out
         turn_s(2, 0, 2)
         turn_pe(2, 4, 2)
         weights_quant(1, 0, 2)
+        fix1(12, 24)
         weights_quant(1, 2, 1)
-        fixv(12, 24)
+        fix2(12, 24)
         store0(1)
         quant_a(3)
         mm(3)
@@ -463,9 +470,10 @@ def tile_head_kernel(tc, f0, f1, f2, w0, b0, w1, b1, w2, b2, anchors, out_0, out
         badd(2, 2)
         sig(24, 36)
         weights_quant(2, 0, 4)
-        fixv(24, 36)
-        store0(2)
+        fix1(24, 36)
         weights_quant(2, 4, 2)
+        fix2(24, 36)
+        store0(2)
         quant5()
         mm(5)
         inter_g(4)
@@ -478,17 +486,19 @@ def tile_head_kernel(tc, f0, f1, f2, w0, b0, w1, b1, w2, b2, anchors, out_0, out
         sig(36, 48)
         quant_b(4)
         cast(32, 36, True)
-        fixv(36, 48)
-        store0(3)
+        fix1(36, 48)
         quant_a(4)
         mm(4)
+        fix2(36, 48)
+        store0(3)
         cast(24, 32, False)
         store1(2)
         badd5()
         sig(-1, 0)
         cast(36, 48, True)
         store1(3)
-        fixv(-1, 0)
+        fix1(-1, 0)
+        fix2(-1, 0)
         store0_5(0)
         store0_5(1)
         cast(-1, 0, False)
@@ -497,14 +507,17 @@ def tile_head_kernel(tc, f0, f1, f2, w0, b0, w1, b1, w2, b2, anchors, out_0, out
         sig(48, 52)
         badd(4, 1)
         sig(52, 56)
-        fixv(48, 52)
+        fix1(48, 52)
+        fix2(48, 52)
         store0(4, 0, 1)
         badd(4, 2)
         sig(56, 60)
-        fixv(52, 56)
+        fix1(52, 56)
+        fix2(52, 56)
         store0(4, 1, 2)
         cast(48, 52, True)
-        fixv(56, 60)
+        fix1(56, 60)
+        fix2(56, 60)
         store0(4, 2, 3)
         cast(52, 56, False)
         cast(56, 60, True)

@@ -482,15 +482,19 @@ def tile_head_kernel(tc, f0, f1, f2, w0, b0, w1, b1, w2, b2, anchors, out_0, out
         store1(1)
         badd(3, 0)
         badd(3, 1)
+        sig(36, 44)
         badd(3, 2)
-        sig(36, 48)
+        sig(44, 48)
+        fix1(36, 44)
         quant_b(4)
+        fix2(36, 44)
+        store0(3, 0, 2)
         cast(32, 36, True)
-        fix1(36, 48)
+        fix1(44, 48)
         quant_a(4)
         mm(4)
-        fix2(36, 48)
-        store0(3)
+        fix2(44, 48)
+        store0(3, 2, 3)
         cast(24, 32, False)
         store1(2)
         badd5()

from contextlib import ExitStack

import concourse.mybir as mybir
from concourse.masks import make_identity

FLOPS = 1107296256

F32 = mybir.dt.float32
BF16 = mybir.dt.bfloat16
I32 = mybir.dt.int32
U32 = mybir.dt.uint32
U8 = mybir.dt.uint8
FP8X4 = mybir.dt.float8_e4m3fn_x4
FP8 = mybir.dt.float8_e4m3fn
ACT = mybir.ActivationFunctionType
ALU = mybir.AluOpType

P = 128
NA = 3
NO = 128
Y_SCALE = 190.0


def tile_head_kernel(tc, f0, f1, f2, w0, b0, w1, b1, w2, b2, anchors, out_0, out_1):
    nc = tc.nc
    with ExitStack() as ctx:
        keep = ctx.enter_context(tc.tile_pool(name="keep", bufs=1))
        ps = ctx.enter_context(tc.psum_pool(name="ps", bufs=1))
        ctx.enter_context(tc.manual_schedule())

        raw00 = keep.tile([P, 4, 512], BF16, name="raw00")
        raw01 = keep.tile([P, 4, 512], BF16, name="raw01")
        raw1x = keep.tile([P, 4, 1024], BF16, name="raw1x")
        wr0 = keep.tile([P, NA, 512], BF16, name="wr0")
        wr1 = keep.tile([P, NA, 512], BF16, name="wr1")
        wr2 = keep.tile([P, NA, 1024], BF16, name="wr2")
        rawl1 = keep.tile([P, 2, 4, 256], BF16, name="rawl1")
        rawl2 = keep.tile([P, 2, 2, 4, 64], BF16, name="rawl2")
        rows_a = keep.tile([P, 416], BF16, name="rows_a")
        rows_b = keep.tile([P, 672], BF16, name="rows_b")
        ones = keep.tile([P, P], BF16, name="ones")
        halves = keep.tile([P, P], BF16, name="halves")
        ident = keep.tile([P, P], F32, name="ident")
        fq2 = keep.tile([P, 576], U32, name="fq2", align_bytes=64)
        fs2 = keep.tile([P, 576], U8, name="fs2", align_bytes=64)
        warm = keep.tile([P, 2], F32, name="warm")

        nc.gpsimd.memset(rows_a[:].bitcast(F32), 0.0)
        make_identity(nc, ident[:])
        nc.gpsimd.memset(ones[:], 1.0)
        nc.gpsimd.memset(rows_b[:].bitcast(F32), 0.0)
        nc.gpsimd.memset(halves[:], 0.0)
        nc.gpsimd.memset(halves[0:64, 0:64], 1.0)
        nc.gpsimd.memset(halves[64:128, 64:128], 1.0)
        nc.vector.memset(warm[:], 0.0)
        nc.vector.memset(fq2[:].bitcast(I32), 0)
        nc.vector.memset(fs2[:].bitcast(I32), 0)
        nc.scalar.activation(out=warm[:, 1:2], in_=warm[:, 0:1], func=ACT.Sigmoid)

        f0n0 = f0[0].rearrange("(p j) u v -> p j (u v)", j=4)
        f0n1 = f0[1].rearrange("(p j) u v -> p j (u v)", j=4)
        anc = anchors.rearrange("(o l) a w -> o (l a w)", o=1)
        w0v = w0.rearrange("(a r) k -> r a k", a=NA)
        nc.sync.dma_start(out=wr0[:, 0:2], in_=w0v[:, 0:2])
        nc.sync.dma_start(out=raw00[:], in_=f0n0[:, :, 0:512])
        nc.sync.dma_start(out=wr0[:, 2:3], in_=w0v[:, 2:3])
        nc.sync.dma_start(out=rows_a[0:1, 0:384], in_=b0.rearrange("(o c) -> o c", o=1))
        nc.sync.dma_start(out=rows_a[0:1, 384:400], in_=anc[:, 0:16])
        nc.sync.dma_start(out=raw01[:], in_=f0n0[:, :, 512:1024])
        nc.sync.dma_start(out=raw1x[:], in_=f0n1)
        nc.sync.dma_start(out=rows_b[0:1, 0:384], in_=b1.rearrange("(o c) -> o c", o=1))
        nc.sync.dma_start(out=rows_b[0:1, 384:640], in_=b2[0:256].rearrange("(o c) -> o c", o=1))
        nc.sync.dma_start(out=rows_b[64:65, 384:640], in_=b2[128:384].rearrange("(o c) -> o c", o=1))
        nc.sync.dma_start(out=rows_b[0:1, 640:644], in_=anc[:, 12:16])
        nc.sync.dma_start(out=rows_b[64:65, 640:644], in_=anc[:, 14:18])
        nc.sync.dma_start(out=wr1[:], in_=w1.rearrange("(a r) k -> r a k", a=NA))
        nc.sync.dma_start(
            out=rawl1[:].rearrange("p n j x -> p n (j x)"),
            in_=f1.rearrange("n (p j) u v -> p n (j u v)", j=4),
        )
        nc.sync.dma_start(out=wr2[:], in_=w2.rearrange("(a r) k -> r a k", a=NA))
        for n in range(2):
            nc.sync.dma_start(
                out=rawl2[:, n].rearrange("p k j x -> p k (j x)"),
                in_=f2[n].rearrange("(k p j) u v -> p k (j u v)", k=2, j=4),
            )

        bias = keep.tile([P, 1024], BF16, name="bias")
        a4 = keep.tile([P, 24, 2], F32, name="a4")
        a45 = keep.tile([P, 4, 2], F32, name="a45")

        def times4(dst, src):
            nc.scalar.activation(out=dst, in_=src, func=ACT.Copy, scale=4.0)

        held = {}
        xt_count = [0]

        def xt_tile(shape, dtype):
            xt_count[0] += 1
            xt = ps.tile(shape, dtype, tag="x%d" % (xt_count[0] % 2))
            return xt

        def spread_a_pe():
            pb = xt_tile([P, 384], BF16)
            nc.tensor.matmul(out=pb[:], lhsT=ones[:], rhs=rows_a[:, 0:384], start=True, stop=True)
            pa = xt_tile([P, 12], F32)
            nc.tensor.matmul(out=pa[:], lhsT=ones[:], rhs=rows_a[:, 384:396], start=True, stop=True)
            held["pb_a"] = pb
            held["pa_a"] = pa

        def spread_a_s():
            pb = held["pb_a"]
            pa = held["pa_a"]
            nc.scalar.copy(out=bias[:, 0:384], in_=pb[:])
            lv0 = pa[:, 0:6].rearrange("p (a w) -> p a w", w=2).unsqueeze(2).to_broadcast([P, NA, 4, 2])
            lv1 = pa[:, 6:12].rearrange("p (a w) -> p a w", w=2).unsqueeze(2).to_broadcast([P, NA, 4, 2])
            times4(a4[:, 0:12, :].rearrange("p (a g) w -> p a g w", g=4), lv0)
            times4(a4[:, 12:24, :].rearrange("p (a g) w -> p a g w", g=4), lv1)

        def spread_b_pe():
            pb = xt_tile([P, 640], BF16)
            nc.tensor.matmul(out=pb[:, 0:384], lhsT=ones[:], rhs=rows_b[:, 0:384], start=True, stop=True)
            nc.tensor.matmul(out=pb[:, 384:640], lhsT=halves[:], rhs=rows_b[:, 384:640], start=True, stop=True)
            pa = xt_tile([P, 4], F32)
            nc.tensor.matmul(out=pa[:], lhsT=halves[:], rhs=rows_b[:, 640:644], start=True, stop=True)
            held["pb_b"] = pb
            held["pa_b"] = pa

        def spread_b_s():
            pb = held["pb_b"]
            pa = held["pa_b"]
            nc.scalar.copy(out=bias[:, 384:1024], in_=pb[:])
            times4(a45[:, 0:2, :], pa[:, 0:2].unsqueeze(1).to_broadcast([P, 2, 2]))
            times4(a45[:, 2:4, :], pa[:, 2:4].unsqueeze(1).to_broadcast([P, 2, 2]))

        wraws = [wr0, wr1, wr2]
        wq = []
        ws = []
        wgs = []
        for lv in range(3):
            units = 3 if lv < 2 else 6
            wg_t = keep.tile([P, units, NO, 4], BF16, name="wg%d" % lv, align_bytes=64)
            wq_t = keep.tile([P, units * NO], U32, name="wq%d" % lv, align_bytes=64)
            ws_t = keep.tile([P, units * NO], U8, name="ws%d" % lv, align_bytes=64)
            wgs.append(wg_t)
            wq.append(wq_t)
            ws.append(ws_t)

        def turn_pe(lv, q0, nq):
            words = wraws[lv][:].bitcast(F32)
            xt = xt_tile([P, 2, 2, NO], F32)
            for i in range(nq):
                kp, a = divmod(q0 + i, NA)
                for u in range(2):
                    nc.tensor.transpose(
                        xt[:, i, u, :], words[:, a, 256 * kp + u : 256 * (kp + 1) : 2], ident[:]
                    )
            held[(lv, q0)] = xt

        def turn_s(lv, q0, nq):
            xt = held[(lv, q0)]
            nc.scalar.copy(
                out=wgs[lv][:].bitcast(F32)[:, q0 : q0 + nq],
                in_=xt[:, 0:nq].rearrange("p i u r -> p i r u"),
            )

        def weights_quant(lv, q0, nq):
            flat = wgs[lv][:].rearrange("p q r t -> p (q r t)")
            nc.vector.quantize_mx(
                out=wq[lv][:, q0 * NO : (q0 + nq) * NO].bitcast(FP8X4),
                scales=ws[lv][:, q0 * NO : (q0 + nq) * NO],
                in_=flat[:, q0 * 4 * NO : (q0 + nq) * 4 * NO],
            )

        fg0 = keep.tile([P, 4, P, 4], BF16, name="fg0", align_bytes=64)
        fg1 = keep.tile([P, 4, P, 4], BF16, name="fg1", align_bytes=64)
        fgb = {}
        fq = []
        fs = []
        for c in range(5):
            if c > 1:
                fgb_t = keep.tile([P, 2, P, 4], BF16, name="fgb_%d" % c, align_bytes=64)
                fgb[c] = fgb_t
            fq_t = keep.tile([P, 512], U32, name="fq_%d" % c, align_bytes=64)
            fs_t = keep.tile([P, 512], U8, name="fs_%d" % c, align_bytes=64)
            fq.append(fq_t)
            fs.append(fs_t)
        og = keep.tile([P, 60, NO], F32, name="og")
        qg = keep.tile([P, 60 * NO], FP8, name="qg")
        og5 = keep.tile([P, 4, NO], F32, name="og5")
        qg5 = keep.tile([P, 4 * NO], FP8, name="qg5")

        def walk(dst, src, g):
            return (dst.rearrange("p g m j -> p m j g"), src.rearrange("p j (m g) -> p m j g", g=g))

        def half(c, h):
            dst = (fg1[:, 0:2] if h == 0 else fgb[c][:]).rearrange("p g m j -> p m j g")
            if c != 3:
                src = raw1x[:, :, 0:512] if c == 2 else raw1x[:, :, 512:1024]
                return (dst, src.rearrange("p j (m g) -> p m j g", g=4)[:, :, :, 2 * h : 2 * h + 2])
            return (dst, rawl1[:, h].rearrange("p j (m g) -> p m j g", g=2))

        def inter0_v():
            o_ap, i_ap = walk(fg0[:, :, 0:64, :], raw00[:, :, 0:256], 4)
            nc.vector.tensor_copy(out=o_ap, in_=i_ap)

        def inter0_b(on_vector):
            o_ap, i_ap = walk(fg0[:, :, 64:128, :], raw00[:, :, 256:512], 4)
            if on_vector:
                nc.vector.tensor_copy(out=o_ap, in_=i_ap)
            else:
                nc.scalar.copy(out=o_ap, in_=i_ap)

        def inter1(h, on_vector):
            o_ap = fg1[:, 2 * h : 2 * h + 2].rearrange("p g m j -> p m j g")
            i_ap = raw01[:].rearrange("p j (m g) -> p m j g", g=4)[:, :, :, 2 * h : 2 * h + 2]
            if on_vector:
                nc.vector.tensor_copy(out=o_ap, in_=i_ap)
            else:
                nc.scalar.copy(out=o_ap, in_=i_ap)

        def inter_g(c):
            o_ap, i_ap = half(c, 0)
            nc.gpsimd.tensor_scalar(out=o_ap, in0=i_ap, scalar1=1.0, scalar2=0.0, op0=ALU.mult, op1=ALU.add)

        def inter_s(c):
            o_ap, i_ap = half(c, 1)
            nc.scalar.copy(out=o_ap, in_=i_ap)

        def inter5_g():
            dst = fg1[:, 0:2].rearrange("p g m j -> p (g m j)").rearrange("p (q x j) -> p q x j", q=4, j=4)
            nc.gpsimd.tensor_scalar(
                out=dst,
                in0=rawl2[:].rearrange("p n k j x -> p (n k) x j"),
                scalar1=1.0,
                scalar2=0.0,
                op0=ALU.mult,
                op1=ALU.add,
            )

        def quant5():
            flat = fg1[:, 0:2].rearrange("p g m j -> p (g m j)")
            for q in range(4):
                c0 = (2 * q + 1) * 64
                nc.vector.quantize_mx(
                    out=fq2[:, c0 : c0 + 64].bitcast(FP8X4),
                    scales=fs2[:, c0 : c0 + 64],
                    in_=flat[:, 256 * q : 256 * (q + 1)],
                )

        def quant(c):
            if c < 2:
                nc.vector.quantize_mx(
                    out=fq[c][:].bitcast(FP8X4), scales=fs[c][:], in_=[fg0, fg1][c][:].rearrange("p g m j -> p (g m j)")
                )

        def quant_b(c):
            nc.vector.quantize_mx(
                out=fq[c][:, 256:512].bitcast(FP8X4),
                scales=fs[c][:, 256:512],
                in_=fgb[c][:].rearrange("p g m j -> p (g m j)"),
            )

        def quant_a(c):
            nc.vector.quantize_mx(
                out=fq[c][:, 0:256].bitcast(FP8X4),
                scales=fs[c][:, 0:256],
                in_=fg1[:, 0:2].rearrange("p g m j -> p (g m j)"),
            )

        banks = {}

        def mm(c):
            if c < 5:
                lv = 1 if c == 3 else 0
                for a in range(NA):
                    acc = ps.tile([P, 4, NO], F32, tag="%s%d" % ("eo"[c % 2], a))
                    for s in range(4):
                        nc.tensor.matmul_mx(
                            out=acc[:, s, :],
                            lhsT=fq[c][:, s * P : (s + 1) * P].bitcast(FP8X4),
                            lhsT_scale=fs[c][:, s * P : (s + 1) * P],
                            rhs=wq[lv][:, a * NO : (a + 1) * NO].bitcast(FP8X4),
                            rhs_scale=ws[lv][:, a * NO : (a + 1) * NO],
                            start=True,
                            stop=True,
                        )
                    banks[(c, a)] = acc
            else:
                acc = xt_tile([P, 2, 2, NO], F32)
                for t in range(2):
                    for n in range(2):
                        todo = []
                        for hf in range(2):
                            for kp in range(2):
                                todo.append(((2 * (2 * n + kp) + 1 - hf) * 64, (kp * NA + t + hf) * NO))
                        for i in range(4):
                            fc, wc = todo[i]
                            nc.tensor.matmul_mx(
                                out=acc[:, t, n, :],
                                lhsT=fq2[:, fc : fc + P].bitcast(FP8X4),
                                lhsT_scale=fs2[:, fc : fc + P],
                                rhs=wq[2][:, wc : wc + NO].bitcast(FP8X4),
                                rhs_scale=ws[2][:, wc : wc + NO],
                                start=(i == 0),
                                stop=(i == 3),
                            )
                banks[5] = acc

        def badd(c, a):
            col = (384 if c == 3 else 0) + a * NO
            nc.vector.tensor_tensor(
                out=og[:, 12 * c + 4 * a : 12 * c + 4 * a + 4, :],
                in0=banks[(c, a)][:],
                in1=bias[:, col : col + NO].unsqueeze(1).to_broadcast([P, 4, NO]),
                op=ALU.add,
            )

        def badd5():
            nc.vector.tensor_tensor(
                out=og5[:].rearrange("p (t n) j -> p t n j", t=2),
                in0=banks[5][:],
                in1=bias[:, 768:1024].rearrange("p (t j) -> p t j", t=2).unsqueeze(2).to_broadcast([P, 2, 2, NO]),
                op=ALU.add,
            )

        sgs = {}

        def sig(r0, r1):
            n = r1 - r0 if r0 >= 0 else 4
            sg = keep.tile([P, n, 4], F32, name="sg%d" % (r0 + 1))
            src = og[:, r0:r1, 0:4] if r0 >= 0 else og5[:, :, 0:4]
            nc.scalar.activation(out=sg[:], in_=src, func=ACT.Sigmoid)
            sgs[r0] = sg

        sas = {}

        def fix1(r0, r1):
            sg = sgs[r0]
            if r0 >= 0:
                rv = og[:, r0:r1]
                z = r0 % 12 + (12 if r0 // 12 == 3 else 0)
                av = a4[:, z : z + r1 - r0, :]
            else:
                rv = og5[:]
                av = a45[:]
            n = r1 - r0 if r0 >= 0 else 4
            sa = keep.tile([P, n, 2], F32, name="sa%d" % (r0 + 1))
            nc.vector.tensor_tensor(out=sa[:], in0=sg[:, :, 2:4], in1=av, op=ALU.mult)
            nc.vector.tensor_scalar(
                out=rv[:, :, 0:2], in0=sg[:, :, 0:2], scalar1=2.0, scalar2=-0.5, op0=ALU.mult, op1=ALU.add
            )
            sas[r0] = sa

        def fix2(r0, r1):
            rv = og[:, r0:r1] if r0 >= 0 else og5[:]
            nc.vector.tensor_tensor(out=rv[:, :, 2:4], in0=sas[r0][:], in1=sgs[r0][:, :, 2:4], op=ALU.mult)

        def cast(r0, r1, on_vector):
            if r0 >= 0:
                src = og[:].rearrange("p r j -> p (r j)")[:, r0 * NO : r1 * NO]
                dst = qg[:, r0 * NO : r1 * NO]
            else:
                src = og5[:].rearrange("p r j -> p (r j)")
                dst = qg5[:]
            if on_vector:
                nc.vector.tensor_scalar(
                    out=dst, in0=src, scalar1=Y_SCALE, scalar2=None, op0=ALU.mult, saturate=False
                )
            else:
                nc.scalar.activation(out=dst, in_=src, func=ACT.Copy, scale=Y_SCALE, saturate=False)

        def stores(c, out, flat, a0, a1):
            na = a1 - a0
            part = flat[:, (12 * c + 4 * a0) * NO : (12 * c + 4 * a1) * NO]
            if c != 3:
                n, h = divmod(min(c, 3), 2)
                v = out[n, 0:3072, :].rearrange("(a h m g) j -> h m a (g j)", a=NA, h=2, m=P, g=4)
                nc.sync.dma_start(out=v[h][:, a0:a1], in_=part.rearrange("p (a x) -> p a x", a=na))
            else:
                s = part.rearrange("p (a n x) -> p n a x", a=na, n=2)
                for n in range(2):
                    nc.sync.dma_start(
                        out=out[n, 3072:3840, :].rearrange("(a m g) j -> m a (g j)", a=NA, m=P, g=2)[:, a0:a1],
                        in_=s[:, n],
                    )

        def stores5(t, out, flat):
            r0 = 3840 + 64 * t
            nc.sync.dma_start(
                out=out[:, r0 : r0 + P, :].rearrange("n m j -> m n j"),
                in_=flat[:, 2 * t * NO : (2 * t + 2) * NO].rearrange("p (n j) -> p n j", n=2),
            )

        def store0(c, a0=0, a1=NA):
            stores(c, out_0, og[:].rearrange("p r j -> p (r j)"), a0, a1)

        def store1(c, a0=0, a1=NA):
            stores(c, out_1, qg[:].bitcast(U8), a0, a1)

        def store0_5(t):
            if t == 0:
                stores5(0, out_0, og5[:].rearrange("p r j -> p (r j)"))
            else:
                nc.sync.dma_start(out=out_0[:, 3968:4032, :].rearrange("n m j -> m n j"), in_=og5[64:128, 2:4, :])

        def store1_5(t):
            stores5(t, out_1, qg5[:].bitcast(U8))

        turn_pe(0, 0, 2)
        turn_pe(0, 2, 1)
        turn_s(0, 0, 2)
        turn_s(0, 2, 1)
        inter0_v()
        weights_quant(0, 0, 2)
        inter0_b(True)
        weights_quant(0, 2, 1)
        spread_a_pe()
        spread_a_s()
        quant(0)
        mm(0)
        spread_b_pe()
        inter1(1, False)
        inter1(0, True)
        quant(1)
        mm(1)
        inter_s(2)
        inter_g(2)
        spread_b_s()
        turn_pe(1, 0, 2)
        turn_pe(1, 2, 1)
        badd(0, 0)
        badd(0, 1)
        badd(0, 2)
        sig(0, 12)
        quant_b(2)
        inter_s(3)
        fix1(0, 12)
        quant_a(2)
        mm(2)
        fix2(0, 12)
        store0(0)
        inter_g(3)
        turn_s(1, 0, 2)
        turn_pe(2, 0, 2)
        turn_s(1, 2, 1)
        turn_pe(2, 2, 2)
        cast(0, 4, False)
        badd(1, 0)
        badd(1, 1)
        badd(1, 2)
        sig(12, 24)
        quant_b(3)
        turn_s(2, 0, 2)
        turn_pe(2, 4, 2)
        weights_quant(1, 0, 2)
        fix1(12, 24)
        weights_quant(1, 2, 1)
        fix2(12, 24)
        store0(1)
        quant_a(3)
        mm(3)
        inter5_g()
        turn_s(2, 2, 2)
        cast(4, 12, False)
        store1(0)
        turn_s(2, 4, 2)
        badd(2, 0)
        badd(2, 1)
        badd(2, 2)
        sig(24, 36)
        weights_quant(2, 0, 4)
        fix1(24, 36)
        weights_quant(2, 4, 2)
        fix2(24, 36)
        store0(2)
        quant5()
        mm(5)
        inter_g(4)
        inter_s(4)
        cast(12, 24, False)
        store1(1)
        badd(3, 0)
        badd(3, 1)
        sig(36, 44)
        badd(3, 2)
        sig(44, 48)
        fix1(36, 44)
        quant_b(4)
        fix2(36, 44)
        store0(3, 0, 2)
        cast(32, 36, True)
        fix1(44, 48)
        quant_a(4)
        mm(4)
        fix2(44, 48)
        store0(3, 2, 3)
        cast(24, 32, False)
        store1(2)
        badd5()
        sig(-1, 0)
        cast(36, 48, True)
        store1(3)
        fix1(-1, 0)
        fix2(-1, 0)
        store0_5(0)
        store0_5(1)
        cast(-1, 0, False)
        store1_5(0)
        badd(4, 0)
        sig(48, 52)
        badd(4, 1)
        sig(52, 56)
        fix1(48, 52)
        fix2(48, 52)
        store0(4, 0, 1)
        badd(4, 2)
        sig(56, 60)
        fix1(52, 56)
        fix2(52, 56)
        store0(4, 1, 2)
        cast(48, 52, True)
        fix1(56, 60)
        fix2(56, 60)
        store0(4, 2, 3)
        cast(52, 56, False)
        cast(56, 60, True)
        store1(4)
        store1_5(1)
